import numpy as np
import ml_dtypes


def mxq(x, axis, fmt="e4m3"):
    dtype, down = {"e4m3": (ml_dtypes.float8_e4m3fn, 7), "e5m2": (ml_dtypes.float8_e5m2, 14)}[fmt]
    v = np.moveaxis(np.asarray(x, np.float32).astype(ml_dtypes.bfloat16).astype(np.float64), axis, -1)
    blocks = v.reshape(v.shape[:-1] + (-1, 32))
    amax = np.abs(blocks).max(-1, keepdims=True)
    byte = np.maximum(np.where(amax > 0, np.frexp(amax)[1] - 1 + 127, 0) - down, 1)
    scale = np.exp2(byte - 127.0)
    codes = (blocks / scale).astype(np.float32).astype(dtype).astype(np.float64)
    return np.moveaxis((codes * scale).reshape(v.shape), -1, axis)


WIDE = False


def mx_kscale(k):
    if not WIDE:
        return np.ones(k)
    levels = np.array([10, -10, 5, -5, 0])
    a = np.random.permutation(np.resize(levels, k // 512 * 4)).reshape(k // 512, 4)
    idx = np.arange(k)
    return np.exp2(a[idx // 512, idx % 128 // 32])


BF16 = ml_dtypes.bfloat16


def bf(x):
    return np.asarray(x, np.float32).astype(BF16)


def f64(x):
    return np.asarray(x).astype(np.float64)


E2M1 = np.array([0.0, 0.5, 1.0, 1.5, 2.0, 3.0, 4.0, 6.0, -0.0, -0.5, -1.0, -1.5, -2.0, -3.0, -4.0, -6.0])


def pack_weight(w, fmt):
    k, n = w.shape
    w = f64(bf(w)).reshape(k // 32, 32, n)
    amax = np.abs(w).max(1)
    if fmt == "e4m3":
        byte = np.frexp(amax)[1] - 1 + 127 - 7
    else:
        mant, ex = np.frexp(amax / 6.0)
        byte = np.where(mant > 0.5, ex, ex - 1) + 127
    byte = np.clip(np.where(amax > 0, byte, 1), 1, 254)
    scaled = (w * np.exp2(127.0 - byte)[:, None, :]).reshape(k, n).astype(np.float32)
    by_word = np.ascontiguousarray(scaled.reshape(k // 512, 128, 4, n).transpose(0, 1, 3, 2))
    if fmt == "e4m3":
        words = by_word.astype(ml_dtypes.float8_e4m3fn).view(np.uint8)
    else:
        c = by_word.astype(ml_dtypes.float4_e2m1fn).view(np.uint8) & 0xF
        words = c[..., 0::2] | (c[..., 1::2] << 4)
    return np.ascontiguousarray(words), np.ascontiguousarray(byte.astype(np.uint8).reshape(k // 512, 16, n))


def unpack_weight(words, scales, fmt):
    g, p, n, _ = words.shape
    if fmt == "e4m3":
        vals = np.ascontiguousarray(words).view(ml_dtypes.float8_e4m3fn).astype(np.float64)
    else:
        nib = np.empty((g, p, n, 4), np.uint8)
        nib[..., 0::2] = words & 0xF
        nib[..., 1::2] = words >> 4
        vals = E2M1[nib]
    vals = vals * np.repeat(np.exp2(scales.astype(np.float64) - 127.0), 8, axis=1)[..., None]
    return vals.transpose(0, 1, 3, 2).reshape(g * 512, n)


B, C, HH, WW, NH, HD, F = 4, 512, 16, 16, 8, 64, 2048
E = NH * HD


def setup_inputs():
    s, t = mx_kscale(E), mx_kscale(C)
    o = bf(np.random.standard_normal((B, HH, WW, E)) * 0.6 * s)
    xn = bf(np.random.standard_normal((B, HH, WW, C)) * 0.5 * t)
    W_O_words, W_O_scales = pack_weight(np.random.standard_normal((E, C)) / np.sqrt(E) / s[:, None] * t, "e4m3")
    scale_attn = bf(0.5 * (1.0 + 0.1 * np.random.standard_normal(1)))
    ffn1_w_words, ffn1_w_scales = pack_weight((np.random.standard_normal((F, C)) * 3.0 / np.sqrt(C) / t).T, "e4m3")
    ffn1_b = bf(np.random.standard_normal(F) * 0.3)
    scale_ffn = bf(0.1 * (1.0 + 0.1 * np.random.standard_normal(1)))
    return {"o": o,
            "xn": xn,
            "W_O_words": W_O_words,
            "W_O_scales": W_O_scales,
            "scale_attn": scale_attn,
            "ffn1_w_words": ffn1_w_words,
            "ffn1_w_scales": ffn1_w_scales,
            "ffn1_b": ffn1_b,
            "scale_ffn": scale_ffn}


def reference(o, xn, W_O_words, W_O_scales, scale_attn, ffn1_w_words, ffn1_w_scales, ffn1_b, scale_ffn):
    p = (mxq(f64(o), 3, "e4m3") @ unpack_weight(W_O_words, W_O_scales, "e4m3")) * f64(scale_attn)
    y = np.maximum(f64(xn) + p, 0.0)
    u = (mxq(y, 3, "e4m3") @ unpack_weight(ffn1_w_words, ffn1_w_scales, "e4m3")) + f64(ffn1_b)
    return np.maximum(u * f64(scale_ffn), 0.0)

@@ -1,0 +1,200 @@
+from contextlib import ExitStack
+
+import concourse.mybir as mybir
+from concourse.masks import make_identity
+
+F32 = mybir.dt.float32
+BF16 = mybir.dt.bfloat16
+I32 = mybir.dt.int32
+U32 = mybir.dt.uint32
+U8 = mybir.dt.uint8
+FP8X4 = mybir.dt.float8_e4m3fn_x4
+ALU = mybir.AluOpType
+ACT = mybir.ActivationFunctionType
+
+P = 128
+PACK = 4
+K = P * PACK
+TOKENS = 1024
+TILES = TOKENS // P
+PAIR = 2
+PAIRS = TILES // PAIR
+CH = 512
+FF = 2048
+BANK = 512
+HALF = 2 * BANK
+QUADRANTS = 4
+
+FLOPS = 2 * TOKENS * K * (CH + FF)
+
+
+def tile_transformerconvblock_pb_kernel(
+    tc, o, xn, W_O_words, W_O_scales, scale_attn, ffn1_w_words, ffn1_w_scales, ffn1_b, scale_ffn, out
+):
+    nc = tc.nc
+    o_dram = o.flatten_outer_dims().rearrange("(p j) k -> p j k", j=TILES)
+    xn_dram = xn.flatten_outer_dims().rearrange("(p j) c -> p j c", j=TILES)
+    out_dram = out.flatten_outer_dims().rearrange("(p j) f -> p j f", j=TILES)
+
+    with ExitStack() as ctx:
+        keep = ctx.enter_context(tc.tile_pool(name="keep", bufs=1))
+        h_pool = ctx.enter_context(tc.tile_pool(name="h_pool", bufs=TILES))
+        psum_turn = ctx.enter_context(tc.psum_pool(name="psum_turn", bufs=2))
+        psum_y = ctx.enter_context(tc.psum_pool(name="psum_y", bufs=2))
+        psum_h = ctx.enter_context(tc.psum_pool(name="psum_h", bufs=4))
+
+        o_rows = keep.tile([P, TILES, K], BF16)
+        xn_rows = keep.tile([P, TILES, CH], BF16)
+        y_rows = keep.tile([P, TILES, CH], BF16)
+        wo_words = keep.tile([P, CH], U32, align_bytes=64)
+        wo_scales = keep.tile([P, CH], U8, align_bytes=64)
+        w1_words = keep.tile([P, FF], U32, align_bytes=64)
+        w1_scales = keep.tile([P, FF], U8, align_bytes=64)
+        o_grouped = keep.tile([P, TILES * P * PACK], BF16, align_bytes=64)
+        y_grouped = keep.tile([P, TILES * P * PACK], BF16, align_bytes=64)
+        o_words = keep.tile([P, TOKENS], U32, align_bytes=64)
+        o_scales = keep.tile([P, TOKENS], U8, align_bytes=64)
+        y_words = keep.tile([P, TOKENS], U32, align_bytes=64)
+        y_scales = keep.tile([P, TOKENS], U8, align_bytes=64)
+
+        nc.vector.memset(wo_scales[:].bitcast(I32), 0)
+        nc.vector.memset(w1_scales[:].bitcast(I32), 0)
+        bias_row = keep.tile([P, FF], BF16)
+        nc.vector.memset(bias_row[:].bitcast(I32), 0)
+        ones = keep.tile([P, P], BF16)
+        nc.vector.memset(ones[:], 1.0)
+        identity = keep.tile([P, P], F32)
+        make_identity(nc, identity[:])
+
+        nc.scalar.dma_start(out=bias_row[0:1, :], in_=ffn1_b.unsqueeze(0))
+        attn_bf16 = keep.tile([P, 1], BF16)
+        nc.scalar.dma_start(out=attn_bf16[:], in_=scale_attn.partition_broadcast(P))
+        ffn_bf16 = keep.tile([P, 1], BF16)
+        nc.scalar.dma_start(out=ffn_bf16[:], in_=scale_ffn.partition_broadcast(P))
+
+        def load_tokens(pair):
+            tiles = slice(pair * PAIR, (pair + 1) * PAIR)
+            nc.sync.dma_start(out=o_rows[:, tiles, :], in_=o_dram[:, tiles, :])
+            nc.sync.dma_start(out=xn_rows[:, tiles, :], in_=xn_dram[:, tiles, :])
+
+        def load_weight(words, scales, words_dram, scales_dram):
+            nc.sync.dma_start(
+                out=words[:].bitcast(I32), in_=words_dram.rearrange("g p n t -> (g p) (n t)").bitcast(I32)
+            )
+            for q in range(QUADRANTS):
+                nc.sync.dma_start(
+                    out=scales[32 * q : 32 * q + 4, :].bitcast(I32),
+                    in_=scales_dram[0, 4 * q : 4 * q + 4, :].bitcast(I32),
+                )
+
+        load_tokens(0)
+        load_weight(wo_words, wo_scales, W_O_words, W_O_scales)
+        load_tokens(1)
+        load_weight(w1_words, w1_scales, ffn1_w_words, ffn1_w_scales)
+        load_tokens(2)
+        load_tokens(3)
+
+        attn = keep.tile([P, 1], F32)
+        nc.vector.tensor_copy(out=attn[:], in_=attn_bf16[:])
+        ffn = keep.tile([P, 1], F32)
+        nc.vector.tensor_copy(out=ffn[:], in_=ffn_bf16[:])
+
+        bias_all = keep.tile([P, FF], BF16)
+        for bank in range(FF // BANK):
+            cols = slice(bank * BANK, (bank + 1) * BANK)
+            spread = psum_h.tile([P, BANK], F32, tag="acc_h")
+            nc.tensor.matmul(spread[:], lhsT=ones[:], rhs=bias_row[:, cols], start=True, stop=True)
+            nc.scalar.copy(out=bias_all[:, cols], in_=spread[:])
+
+        def turn(rows, pair):
+            turned = psum_turn.tile([P, PAIR, 2, P], F32)
+            for i in range(PAIR):
+                words = rows[:, pair * PAIR + i, :].bitcast(F32)
+                for u in range(2):
+                    nc.tensor.transpose(turned[:, i, u, :], words[:, u : K // 2 : 2], identity[:])
+            return turned
+
+        def quantise(grouped, words, scales, pair):
+            cols = slice(pair * PAIR * P, (pair + 1) * PAIR * P)
+            nc.vector.quantize_mx(
+                out=words[:, cols].bitcast(FP8X4),
+                scales=scales[:, cols],
+                in_=grouped[:, pair * PAIR * P * PACK : (pair + 1) * PAIR * P * PACK],
+            )
+
+        def quantise_o(pair):
+            turned = turn(o_rows, pair)
+            nc.scalar.copy(
+                out=o_grouped[:, pair * PAIR * P * PACK : (pair + 1) * PAIR * P * PACK]
+                .bitcast(F32)
+                .rearrange("p (i r u) -> p i r u", i=PAIR, u=2),
+                in_=turned[:].rearrange("p i u r -> p i r u"),
+            )
+            quantise(o_grouped, o_words, o_scales, pair)
+
+        def attention_output(pair):
+            for j in range(pair * PAIR, (pair + 1) * PAIR):
+                tokens = slice(j * P, (j + 1) * P)
+                acc_y = psum_y.tile([P, CH], F32)
+                nc.tensor.matmul_mx(
+                    out=acc_y[:],
+                    lhsT=o_words[:, tokens].bitcast(FP8X4),
+                    lhsT_scale=o_scales[:, tokens],
+                    rhs=wo_words[:].bitcast(FP8X4),
+                    rhs_scale=wo_scales[:],
+                    start=True,
+                    stop=True,
+                )
+                nc.vector.scalar_tensor_tensor(
+                    out=y_rows[:, j, :],
+                    in0=acc_y[:],
+                    scalar=attn[:, 0:1],
+                    in1=xn_rows[:, j, :],
+                    op0=ALU.mult,
+                    op1=ALU.add,
+                )
+
+        def quantise_y(pair):
+            turned = turn(y_rows, pair)
+            for i in range(PAIR):
+                j = pair * PAIR + i
+                nc.scalar.activation(
+                    out=y_grouped[:, j * P * PACK : (j + 1) * P * PACK].rearrange(
+                        "p (r u e) -> p r u e", u=2, e=2
+                    ),
+                    in_=turned[:, i, :, :].bitcast(BF16).rearrange("p u (r e) -> p r u e", e=2),
+                    func=ACT.Relu,
+                )
+            quantise(y_grouped, y_words, y_scales, pair)
+
+        def feed_forward(pair):
+            for j in range(pair * PAIR, (pair + 1) * PAIR):
+                tokens = slice(j * P, (j + 1) * P)
+                h = h_pool.tile([P, FF], F32)
+                for half in range(FF // HALF):
+                    for bank in range(half * HALF // BANK, (half + 1) * HALF // BANK):
+                        cols = slice(bank * BANK, (bank + 1) * BANK)
+                        acc_h = psum_h.tile([P, BANK], F32)
+                        nc.tensor.matmul_mx(
+                            out=acc_h[:],
+                            lhsT=y_words[:, tokens].bitcast(FP8X4),
+                            lhsT_scale=y_scales[:, tokens],
+                            rhs=w1_words[:, cols].bitcast(FP8X4),
+                            rhs_scale=w1_scales[:, cols],
+                            start=True,
+                            stop=True,
+                        )
+                        nc.vector.tensor_tensor(out=h[:, cols], in0=acc_h[:], in1=bias_all[:, cols], op=ALU.add)
+                    cols = slice(half * HALF, (half + 1) * HALF)
+                    nc.scalar.activation(out=h[:, cols], in_=h[:, cols], func=ACT.Relu, scale=ffn[:, 0:1])
+                    nc.sync.dma_start(out=out_dram[:, j, cols], in_=h[:, cols])
+
+        for step in range(PAIRS + 3):
+            if step < PAIRS:
+                quantise_o(step)
+            if 0 <= step - 1 < PAIRS:
+                attention_output(step - 1)
+            if 0 <= step - 2 < PAIRS:
+                quantise_y(step - 2)
+            if 0 <= step - 3 < PAIRS:
+                feed_forward(step - 3)

@@ -1,3 +1,4 @@
+import math
 from contextlib import ExitStack
 
 import concourse.mybir as mybir
@@ -99,12 +100,12 @@ def tile_transformerconvblock_pb_kernel(
         ffn = keep.tile([P, 1], F32)
         nc.vector.tensor_copy(out=ffn[:], in_=ffn_bf16[:])
 
-        bias_all = keep.tile([P, FF], BF16)
+        bias_all = keep.tile([P, FF], F32)
         for bank in range(FF // BANK):
             cols = slice(bank * BANK, (bank + 1) * BANK)
             spread = psum_h.tile([P, BANK], F32, tag="acc_h")
             nc.tensor.matmul(spread[:], lhsT=ones[:], rhs=bias_row[:, cols], start=True, stop=True)
-            nc.scalar.copy(out=bias_all[:, cols], in_=spread[:])
+            nc.scalar.activation(out=bias_all[:, cols], in_=spread[:], func=ACT.Copy, scale=ffn[:, 0:1])
 
         def turn(rows, pair):
             turned = psum_turn.tile([P, PAIR, 2, P], F32)
@@ -184,9 +185,21 @@ def tile_transformerconvblock_pb_kernel(
                             start=True,
                             stop=True,
                         )
-                        nc.vector.tensor_tensor(out=h[:, cols], in0=acc_h[:], in1=bias_all[:, cols], op=ALU.add)
+                        nc.vector.scalar_tensor_tensor(
+                            out=h[:, cols],
+                            in0=acc_h[:],
+                            scalar=ffn[:, 0:1],
+                            in1=bias_all[:, cols],
+                            op0=ALU.mult,
+                            op1=ALU.add,
+                        )
                     cols = slice(half * HALF, (half + 1) * HALF)
-                    nc.scalar.activation(out=h[:, cols], in_=h[:, cols], func=ACT.Relu, scale=ffn[:, 0:1])
+                    if half == 0:
+                        nc.gpsimd.tensor_scalar(
+                            out=h[:, cols], in0=h[:, cols], scalar1=math.inf, scalar2=0.0, op0=ALU.min, op1=ALU.max
+                        )
+                    else:
+                        nc.scalar.activation(out=h[:, cols], in_=h[:, cols], func=ACT.Relu)
                     nc.sync.dma_start(out=out_dram[:, j, cols], in_=h[:, cols])
 
         for step in range(PAIRS + 3):

@@ -1,4 +1,3 @@
-import math
 from contextlib import ExitStack
 
 import concourse.mybir as mybir
@@ -18,8 +17,9 @@ PACK = 4
 K = P * PACK
 TOKENS = 1024
 TILES = TOKENS // P
-PAIR = 2
+PAIR = 1
 PAIRS = TILES // PAIR
+LOAD = 2
 CH = 512
 FF = 2048
 BANK = 512
@@ -73,8 +73,8 @@ def tile_transformerconvblock_pb_kernel(
         ffn_bf16 = keep.tile([P, 1], BF16)
         nc.scalar.dma_start(out=ffn_bf16[:], in_=scale_ffn.partition_broadcast(P))
 
-        def load_tokens(pair):
-            tiles = slice(pair * PAIR, (pair + 1) * PAIR)
+        def load_tokens(part):
+            tiles = slice(part * LOAD, (part + 1) * LOAD)
             nc.sync.dma_start(out=o_rows[:, tiles, :], in_=o_dram[:, tiles, :])
             nc.sync.dma_start(out=xn_rows[:, tiles, :], in_=xn_dram[:, tiles, :])
 
@@ -100,12 +100,12 @@ def tile_transformerconvblock_pb_kernel(
         ffn = keep.tile([P, 1], F32)
         nc.vector.tensor_copy(out=ffn[:], in_=ffn_bf16[:])
 
-        bias_all = keep.tile([P, FF], F32)
+        bias_all = keep.tile([P, FF], BF16)
         for bank in range(FF // BANK):
             cols = slice(bank * BANK, (bank + 1) * BANK)
             spread = psum_h.tile([P, BANK], F32, tag="acc_h")
             nc.tensor.matmul(spread[:], lhsT=ones[:], rhs=bias_row[:, cols], start=True, stop=True)
-            nc.scalar.activation(out=bias_all[:, cols], in_=spread[:], func=ACT.Copy, scale=ffn[:, 0:1])
+            nc.scalar.copy(out=bias_all[:, cols], in_=spread[:])
 
         def turn(rows, pair):
             turned = psum_turn.tile([P, PAIR, 2, P], F32)
@@ -185,21 +185,9 @@ def tile_transformerconvblock_pb_kernel(
                             start=True,
                             stop=True,
                         )
-                        nc.vector.scalar_tensor_tensor(
-                            out=h[:, cols],
-                            in0=acc_h[:],
-                            scalar=ffn[:, 0:1],
-                            in1=bias_all[:, cols],
-                            op0=ALU.mult,
-                            op1=ALU.add,
-                        )
+                        nc.vector.tensor_tensor(out=h[:, cols], in0=acc_h[:], in1=bias_all[:, cols], op=ALU.add)
                     cols = slice(half * HALF, (half + 1) * HALF)
-                    if half == 0:
-                        nc.gpsimd.tensor_scalar(
-                            out=h[:, cols], in0=h[:, cols], scalar1=math.inf, scalar2=0.0, op0=ALU.min, op1=ALU.max
-                        )
-                    else:
-                        nc.scalar.activation(out=h[:, cols], in_=h[:, cols], func=ACT.Relu)
+                    nc.scalar.activation(out=h[:, cols], in_=h[:, cols], func=ACT.Relu, scale=ffn[:, 0:1])
                     nc.sync.dma_start(out=out_dram[:, j, cols], in_=h[:, cols])
 
         for step in range(PAIRS + 3):

@@ -23,7 +23,10 @@ LOAD = 2
 CH = 512
 FF = 2048
 BANK = 512
-HALF = 2 * BANK
+TURNED = 512
+DIRECT = FF - TURNED
+BLOCKS = TURNED // P
+POOL_BANKS = 2
 QUADRANTS = 4
 
 FLOPS = 2 * TOKENS * K * (CH + FF)
@@ -40,9 +43,12 @@ def tile_transformerconvblock_pb_kernel(
     with ExitStack() as ctx:
         keep = ctx.enter_context(tc.tile_pool(name="keep", bufs=1))
         h_pool = ctx.enter_context(tc.tile_pool(name="h_pool", bufs=TILES))
+        t_pool = ctx.enter_context(tc.tile_pool(name="t_pool", bufs=3))
         psum_turn = ctx.enter_context(tc.psum_pool(name="psum_turn", bufs=2))
-        psum_y = ctx.enter_context(tc.psum_pool(name="psum_y", bufs=2))
-        psum_h = ctx.enter_context(tc.psum_pool(name="psum_h", bufs=4))
+        psum_y = ctx.enter_context(tc.psum_pool(name="psum_y", bufs=1))
+        psum_h = ctx.enter_context(tc.psum_pool(name="psum_h", bufs=3))
+        psum_t = ctx.enter_context(tc.psum_pool(name="psum_t", bufs=1))
+        psum_back = ctx.enter_context(tc.psum_pool(name="psum_back", bufs=1))
 
         o_rows = keep.tile([P, TILES, K], BF16)
         xn_rows = keep.tile([P, TILES, CH], BF16)
@@ -67,9 +73,9 @@ def tile_transformerconvblock_pb_kernel(
         identity = keep.tile([P, P], F32)
         make_identity(nc, identity[:])
 
-        nc.scalar.dma_start(out=bias_row[0:1, :], in_=ffn1_b.unsqueeze(0))
         attn_bf16 = keep.tile([P, 1], BF16)
         nc.scalar.dma_start(out=attn_bf16[:], in_=scale_attn.partition_broadcast(P))
+        nc.scalar.dma_start(out=bias_row[0:1, :], in_=ffn1_b.unsqueeze(0))
         ffn_bf16 = keep.tile([P, 1], BF16)
         nc.scalar.dma_start(out=ffn_bf16[:], in_=scale_ffn.partition_broadcast(P))
 
@@ -101,11 +107,26 @@ def tile_transformerconvblock_pb_kernel(
         nc.vector.tensor_copy(out=ffn[:], in_=ffn_bf16[:])
 
         bias_all = keep.tile([P, FF], BF16)
-        for bank in range(FF // BANK):
+
+        def spread_bias(bank):
             cols = slice(bank * BANK, (bank + 1) * BANK)
             spread = psum_h.tile([P, BANK], F32, tag="acc_h")
             nc.tensor.matmul(spread[:], lhsT=ones[:], rhs=bias_row[:, cols], start=True, stop=True)
-            nc.scalar.copy(out=bias_all[:, cols], in_=spread[:])
+            nc.vector.tensor_copy(out=bias_all[:, cols], in_=spread[:])
+
+        bias_turned = keep.tile([P, BLOCKS], F32)
+
+        def turn_bias():
+            column = psum_back.tile([P, BLOCKS], F32, tag="back")
+            for c in range(BLOCKS):
+                nc.tensor.matmul(
+                    column[:, c : c + 1],
+                    lhsT=bias_row[:, DIRECT + c * P : DIRECT + (c + 1) * P],
+                    rhs=ones[:, 0:1],
+                    start=True,
+                    stop=True,
+                )
+            nc.vector.tensor_scalar_mul(out=bias_turned[:], in0=column[:], scalar1=ffn[:, 0:1])
 
         def turn(rows, pair):
             turned = psum_turn.tile([P, PAIR, 2, P], F32)
@@ -168,34 +189,77 @@ def tile_transformerconvblock_pb_kernel(
                 )
             quantise(y_grouped, y_words, y_scales, pair)
 
-        def feed_forward(pair):
-            for j in range(pair * PAIR, (pair + 1) * PAIR):
-                tokens = slice(j * P, (j + 1) * P)
-                h = h_pool.tile([P, FF], F32)
-                for half in range(FF // HALF):
-                    for bank in range(half * HALF // BANK, (half + 1) * HALF // BANK):
-                        cols = slice(bank * BANK, (bank + 1) * BANK)
-                        acc_h = psum_h.tile([P, BANK], F32)
-                        nc.tensor.matmul_mx(
-                            out=acc_h[:],
-                            lhsT=y_words[:, tokens].bitcast(FP8X4),
-                            lhsT_scale=y_scales[:, tokens],
-                            rhs=w1_words[:, cols].bitcast(FP8X4),
-                            rhs_scale=w1_scales[:, cols],
-                            start=True,
-                            stop=True,
-                        )
-                        nc.vector.tensor_tensor(out=h[:, cols], in0=acc_h[:], in1=bias_all[:, cols], op=ALU.add)
-                    cols = slice(half * HALF, (half + 1) * HALF)
-                    nc.scalar.activation(out=h[:, cols], in_=h[:, cols], func=ACT.Relu, scale=ffn[:, 0:1])
-                    nc.sync.dma_start(out=out_dram[:, j, cols], in_=h[:, cols])
+        h_tiles = {}
+        t_tiles = {}
 
-        for step in range(PAIRS + 3):
-            if step < PAIRS:
+        def feed_forward(j):
+            tokens = slice(j * P, (j + 1) * P)
+            h = h_pool.tile([P, FF], F32)
+            h_tiles[j] = h
+            for bank in range(DIRECT // BANK):
+                cols = slice(bank * BANK, (bank + 1) * BANK)
+                acc_h = psum_h.tile([P, BANK], F32)
+                nc.tensor.matmul_mx(
+                    out=acc_h[:],
+                    lhsT=y_words[:, tokens].bitcast(FP8X4),
+                    lhsT_scale=y_scales[:, tokens],
+                    rhs=w1_words[:, cols].bitcast(FP8X4),
+                    rhs_scale=w1_scales[:, cols],
+                    start=True,
+                    stop=True,
+                )
+                nc.vector.tensor_tensor(out=h[:, cols], in0=acc_h[:], in1=bias_all[:, cols], op=ALU.add)
+                if bank < POOL_BANKS:
+                    nc.gpsimd.tensor_scalar(
+                        out=h[:, cols], in0=h[:, cols], scalar1=ffn[:, 0:1], scalar2=0.0, op0=ALU.mult, op1=ALU.max
+                    )
+                else:
+                    nc.scalar.activation(out=h[:, cols], in_=h[:, cols], func=ACT.Relu, scale=ffn[:, 0:1])
+            nc.sync.dma_start(out=out_dram[:, j, 0:DIRECT], in_=h[:, 0:DIRECT])
+            acc_t = psum_t.tile([P, BLOCKS, P], F32)
+            h_turned = t_pool.tile([P, BLOCKS, P], F32)
+            t_tiles[j] = h_turned
+            for c in range(BLOCKS):
+                cols = slice(DIRECT + c * P, DIRECT + (c + 1) * P)
+                nc.tensor.matmul_mx(
+                    out=acc_t[:, c, :],
+                    lhsT=w1_words[:, cols].bitcast(FP8X4),
+                    lhsT_scale=w1_scales[:, cols],
+                    rhs=y_words[:, tokens].bitcast(FP8X4),
+                    rhs_scale=y_scales[:, tokens],
+                    start=True,
+                    stop=True,
+                )
+            for c in range(BLOCKS):
+                nc.scalar.activation(
+                    out=h_turned[:, c, :],
+                    in_=acc_t[:, c, :],
+                    func=ACT.Relu,
+                    bias=bias_turned[:, c : c + 1],
+                    scale=ffn[:, 0:1],
+                )
+
+        def turn_back(j):
+            back = psum_back.tile([P, BLOCKS, P], F32)
+            for c in range(BLOCKS):
+                nc.tensor.transpose(back[:, c, :], t_tiles[j][:, c, :], identity[:])
+            h = h_tiles[j]
+            nc.scalar.copy(out=h[:, DIRECT:FF], in_=back[:].rearrange("p c r -> p (c r)"))
+            nc.sync.dma_start(out=out_dram[:, j, DIRECT:FF], in_=h[:, DIRECT:FF])
+
+        for step in range(TILES + 4):
+            if step < TILES:
                 quantise_o(step)
-            if 0 <= step - 1 < PAIRS:
+            if 0 <= step - 1 < TILES:
                 attention_output(step - 1)
-            if 0 <= step - 2 < PAIRS:
+            if step in (1, 2):
+                for bank in range(2 * (step - 1), min(2 * step, DIRECT // BANK)):
+                    spread_bias(bank)
+            if step == 2:
+                turn_bias()
+            if 0 <= step - 2 < TILES:
                 quantise_y(step - 2)
-            if 0 <= step - 3 < PAIRS:
+            if 0 <= step - 3 < TILES:
                 feed_forward(step - 3)
+            if 0 <= step - 4 < TILES:
+                turn_back(step - 4)

@@ -27,6 +27,7 @@ TURNED = 512
 DIRECT = FF - TURNED
 BLOCKS = TURNED // P
 POOL_BANKS = 2
+LARGEST = 3.0e38
 QUADRANTS = 4
 
 FLOPS = 2 * TOKENS * K * (CH + FF)
@@ -106,13 +107,13 @@ def tile_transformerconvblock_pb_kernel(
         ffn = keep.tile([P, 1], F32)
         nc.vector.tensor_copy(out=ffn[:], in_=ffn_bf16[:])
 
-        bias_all = keep.tile([P, FF], BF16)
+        bias_all = keep.tile([P, DIRECT], F32)
 
         def spread_bias(bank):
             cols = slice(bank * BANK, (bank + 1) * BANK)
             spread = psum_h.tile([P, BANK], F32, tag="acc_h")
             nc.tensor.matmul(spread[:], lhsT=ones[:], rhs=bias_row[:, cols], start=True, stop=True)
-            nc.vector.tensor_copy(out=bias_all[:, cols], in_=spread[:])
+            nc.vector.tensor_scalar_mul(out=bias_all[:, cols], in0=spread[:], scalar1=ffn[:, 0:1])
 
         bias_turned = keep.tile([P, BLOCKS], F32)
 
@@ -208,13 +209,20 @@ def tile_transformerconvblock_pb_kernel(
                     start=True,
                     stop=True,
                 )
-                nc.vector.tensor_tensor(out=h[:, cols], in0=acc_h[:], in1=bias_all[:, cols], op=ALU.add)
+                nc.vector.scalar_tensor_tensor(
+                    out=h[:, cols],
+                    in0=acc_h[:],
+                    scalar=ffn[:, 0:1],
+                    in1=bias_all[:, cols],
+                    op0=ALU.mult,
+                    op1=ALU.add,
+                )
                 if bank < POOL_BANKS:
                     nc.gpsimd.tensor_scalar(
-                        out=h[:, cols], in0=h[:, cols], scalar1=ffn[:, 0:1], scalar2=0.0, op0=ALU.mult, op1=ALU.max
+                        out=h[:, cols], in0=h[:, cols], scalar1=LARGEST, scalar2=0.0, op0=ALU.min, op1=ALU.max
                     )
                 else:
-                    nc.scalar.activation(out=h[:, cols], in_=h[:, cols], func=ACT.Relu, scale=ffn[:, 0:1])
+                    nc.scalar.activation(out=h[:, cols], in_=h[:, cols], func=ACT.Relu)
             nc.sync.dma_start(out=out_dram[:, j, 0:DIRECT], in_=h[:, 0:DIRECT])
             acc_t = psum_t.tile([P, BLOCKS, P], F32)
             h_turned = t_pool.tile([P, BLOCKS, P], F32)

@@ -197,6 +197,28 @@ def tile_transformerconvblock_pb_kernel(
             tokens = slice(j * P, (j + 1) * P)
             h = h_pool.tile([P, FF], F32)
             h_tiles[j] = h
+            acc_t = psum_t.tile([P, BLOCKS, P], F32)
+            h_turned = t_pool.tile([P, BLOCKS, P], F32)
+            t_tiles[j] = h_turned
+            for c in range(BLOCKS):
+                cols = slice(DIRECT + c * P, DIRECT + (c + 1) * P)
+                nc.tensor.matmul_mx(
+                    out=acc_t[:, c, :],
+                    lhsT=w1_words[:, cols].bitcast(FP8X4),
+                    lhsT_scale=w1_scales[:, cols],
+                    rhs=y_words[:, tokens].bitcast(FP8X4),
+                    rhs_scale=y_scales[:, tokens],
+                    start=True,
+                    stop=True,
+                )
+            for c in range(BLOCKS):
+                nc.scalar.activation(
+                    out=h_turned[:, c, :],
+                    in_=acc_t[:, c, :],
+                    func=ACT.Relu,
+                    bias=bias_turned[:, c : c + 1],
+                    scale=ffn[:, 0:1],
+                )
             for bank in range(DIRECT // BANK):
                 cols = slice(bank * BANK, (bank + 1) * BANK)
                 acc_h = psum_h.tile([P, BANK], F32)
@@ -224,28 +246,6 @@ def tile_transformerconvblock_pb_kernel(
                 else:
                     nc.scalar.activation(out=h[:, cols], in_=h[:, cols], func=ACT.Relu)
             nc.sync.dma_start(out=out_dram[:, j, 0:DIRECT], in_=h[:, 0:DIRECT])
-            acc_t = psum_t.tile([P, BLOCKS, P], F32)
-            h_turned = t_pool.tile([P, BLOCKS, P], F32)
-            t_tiles[j] = h_turned
-            for c in range(BLOCKS):
-                cols = slice(DIRECT + c * P, DIRECT + (c + 1) * P)
-                nc.tensor.matmul_mx(
-                    out=acc_t[:, c, :],
-                    lhsT=w1_words[:, cols].bitcast(FP8X4),
-                    lhsT_scale=w1_scales[:, cols],
-                    rhs=y_words[:, tokens].bitcast(FP8X4),
-                    rhs_scale=y_scales[:, tokens],
-                    start=True,
-                    stop=True,
-                )
-            for c in range(BLOCKS):
-                nc.scalar.activation(
-                    out=h_turned[:, c, :],
-                    in_=acc_t[:, c, :],
-                    func=ACT.Relu,
-                    bias=bias_turned[:, c : c + 1],
-                    scale=ffn[:, 0:1],
-                )
 
         def turn_back(j):
             back = psum_back.tile([P, BLOCKS, P], F32)
@@ -255,9 +255,14 @@ def tile_transformerconvblock_pb_kernel(
             nc.scalar.copy(out=h[:, DIRECT:FF], in_=back[:].rearrange("p c r -> p (c r)"))
             nc.sync.dma_start(out=out_dram[:, j, DIRECT:FF], in_=h[:, DIRECT:FF])
 
+        ctx.enter_context(tc.manual_schedule(engines={mybir.EngineType.PE}))
         for step in range(TILES + 4):
             if step < TILES:
                 quantise_o(step)
+            if 0 <= step - 4 < TILES:
+                turn_back(step - 4)
+            if 0 <= step - 2 < TILES:
+                quantise_y(step - 2)
             if 0 <= step - 1 < TILES:
                 attention_output(step - 1)
             if step in (1, 2):
@@ -265,9 +270,5 @@ def tile_transformerconvblock_pb_kernel(
                     spread_bias(bank)
             if step == 2:
                 turn_bias()
-            if 0 <= step - 2 < TILES:
-                quantise_y(step - 2)
             if 0 <= step - 3 < TILES:
                 feed_forward(step - 3)
-            if 0 <= step - 4 < TILES:
-                turn_back(step - 4)

@@ -129,99 +129,77 @@ def tile_transformerconvblock_pb_kernel(
                 )
             nc.vector.tensor_scalar_mul(out=bias_turned[:], in0=column[:], scalar1=ffn[:, 0:1])
 
-        def turn(rows, pair):
-            turned = psum_turn.tile([P, PAIR, 2, P], F32)
-            for i in range(PAIR):
-                words = rows[:, pair * PAIR + i, :].bitcast(F32)
-                for u in range(2):
-                    nc.tensor.transpose(turned[:, i, u, :], words[:, u : K // 2 : 2], identity[:])
+        def turn(rows, j):
+            turned = psum_turn.tile([P, 2, P], F32)
+            words = rows[:, j, :].bitcast(F32)
+            for u in range(2):
+                nc.tensor.transpose(turned[:, u, :], words[:, u : K // 2 : 2], identity[:])
             return turned
 
-        def quantise(grouped, words, scales, pair):
-            cols = slice(pair * PAIR * P, (pair + 1) * PAIR * P)
+        def quantise(grouped, words, scales, j):
             nc.vector.quantize_mx(
-                out=words[:, cols].bitcast(FP8X4),
-                scales=scales[:, cols],
-                in_=grouped[:, pair * PAIR * P * PACK : (pair + 1) * PAIR * P * PACK],
+                out=words[:, j * P : (j + 1) * P].bitcast(FP8X4),
+                scales=scales[:, j * P : (j + 1) * P],
+                in_=grouped[:, j * K : (j + 1) * K],
             )
 
-        def quantise_o(pair):
-            turned = turn(o_rows, pair)
+        o_turned, y_turned, y_sums, h_sums, t_sums, h_tiles, t_tiles, backs = {}, {}, {}, {}, {}, {}, {}, {}
+
+        def o_turn(j):
+            o_turned[j] = turn(o_rows, j)
+
+        def o_copy(j):
             nc.scalar.copy(
-                out=o_grouped[:, pair * PAIR * P * PACK : (pair + 1) * PAIR * P * PACK]
-                .bitcast(F32)
-                .rearrange("p (i r u) -> p i r u", i=PAIR, u=2),
-                in_=turned[:].rearrange("p i u r -> p i r u"),
+                out=o_grouped[:, j * K : (j + 1) * K].bitcast(F32).rearrange("p (r u) -> p r u", u=2),
+                in_=o_turned[j][:].rearrange("p u r -> p r u"),
             )
-            quantise(o_grouped, o_words, o_scales, pair)
 
-        def attention_output(pair):
-            for j in range(pair * PAIR, (pair + 1) * PAIR):
-                tokens = slice(j * P, (j + 1) * P)
-                acc_y = psum_y.tile([P, CH], F32)
-                nc.tensor.matmul_mx(
-                    out=acc_y[:],
-                    lhsT=o_words[:, tokens].bitcast(FP8X4),
-                    lhsT_scale=o_scales[:, tokens],
-                    rhs=wo_words[:].bitcast(FP8X4),
-                    rhs_scale=wo_scales[:],
-                    start=True,
-                    stop=True,
-                )
-                nc.vector.scalar_tensor_tensor(
-                    out=y_rows[:, j, :],
-                    in0=acc_y[:],
-                    scalar=attn[:, 0:1],
-                    in1=xn_rows[:, j, :],
-                    op0=ALU.mult,
-                    op1=ALU.add,
-                )
+        def o_quantise(j):
+            quantise(o_grouped, o_words, o_scales, j)
 
-        def quantise_y(pair):
-            turned = turn(y_rows, pair)
-            for i in range(PAIR):
-                j = pair * PAIR + i
-                nc.scalar.activation(
-                    out=y_grouped[:, j * P * PACK : (j + 1) * P * PACK].rearrange(
-                        "p (r u e) -> p r u e", u=2, e=2
-                    ),
-                    in_=turned[:, i, :, :].bitcast(BF16).rearrange("p u (r e) -> p r u e", e=2),
-                    func=ACT.Relu,
-                )
-            quantise(y_grouped, y_words, y_scales, pair)
-
-        h_tiles = {}
-        t_tiles = {}
-
-        def feed_forward(j):
+        def attention_pass(j):
             tokens = slice(j * P, (j + 1) * P)
-            h = h_pool.tile([P, FF], F32)
-            h_tiles[j] = h
-            acc_t = psum_t.tile([P, BLOCKS, P], F32)
-            h_turned = t_pool.tile([P, BLOCKS, P], F32)
-            t_tiles[j] = h_turned
-            for c in range(BLOCKS):
-                cols = slice(DIRECT + c * P, DIRECT + (c + 1) * P)
-                nc.tensor.matmul_mx(
-                    out=acc_t[:, c, :],
-                    lhsT=w1_words[:, cols].bitcast(FP8X4),
-                    lhsT_scale=w1_scales[:, cols],
-                    rhs=y_words[:, tokens].bitcast(FP8X4),
-                    rhs_scale=y_scales[:, tokens],
-                    start=True,
-                    stop=True,
-                )
-            for c in range(BLOCKS):
-                nc.scalar.activation(
-                    out=h_turned[:, c, :],
-                    in_=acc_t[:, c, :],
-                    func=ACT.Relu,
-                    bias=bias_turned[:, c : c + 1],
-                    scale=ffn[:, 0:1],
-                )
+            acc_y = psum_y.tile([P, CH], F32)
+            y_sums[j] = acc_y
+            nc.tensor.matmul_mx(
+                out=acc_y[:],
+                lhsT=o_words[:, tokens].bitcast(FP8X4),
+                lhsT_scale=o_scales[:, tokens],
+                rhs=wo_words[:].bitcast(FP8X4),
+                rhs_scale=wo_scales[:],
+                start=True,
+                stop=True,
+            )
+
+        def attention_add(j):
+            nc.vector.scalar_tensor_tensor(
+                out=y_rows[:, j, :],
+                in0=y_sums[j][:],
+                scalar=attn[:, 0:1],
+                in1=xn_rows[:, j, :],
+                op0=ALU.mult,
+                op1=ALU.add,
+            )
+
+        def y_turn(j):
+            y_turned[j] = turn(y_rows, j)
+
+        def y_copy(j):
+            nc.scalar.activation(
+                out=y_grouped[:, j * K : (j + 1) * K].rearrange("p (r u e) -> p r u e", u=2, e=2),
+                in_=y_turned[j][:].bitcast(BF16).rearrange("p u (r e) -> p r u e", e=2),
+                func=ACT.Relu,
+            )
+
+        def y_quantise(j):
+            quantise(y_grouped, y_words, y_scales, j)
+
+        def direct_passes(j):
+            tokens = slice(j * P, (j + 1) * P)
             for bank in range(DIRECT // BANK):
                 cols = slice(bank * BANK, (bank + 1) * BANK)
                 acc_h = psum_h.tile([P, BANK], F32)
+                h_sums[j, bank] = acc_h
                 nc.tensor.matmul_mx(
                     out=acc_h[:],
                     lhsT=y_words[:, tokens].bitcast(FP8X4),
@@ -231,9 +209,14 @@ def tile_transformerconvblock_pb_kernel(
                     start=True,
                     stop=True,
                 )
+
+        def direct_out(j):
+            h = h_tiles[j]
+            for bank in range(DIRECT // BANK):
+                cols = slice(bank * BANK, (bank + 1) * BANK)
                 nc.vector.scalar_tensor_tensor(
                     out=h[:, cols],
-                    in0=acc_h[:],
+                    in0=h_sums[j, bank][:],
                     scalar=ffn[:, 0:1],
                     in1=bias_all[:, cols],
                     op0=ALU.mult,
@@ -245,30 +228,71 @@ def tile_transformerconvblock_pb_kernel(
                     )
                 else:
                     nc.scalar.activation(out=h[:, cols], in_=h[:, cols], func=ACT.Relu)
-            nc.sync.dma_start(out=out_dram[:, j, 0:DIRECT], in_=h[:, 0:DIRECT])
+                nc.sync.dma_start(out=out_dram[:, j, cols], in_=h[:, cols])
 
-        def turn_back(j):
+        def turned_passes(j):
+            tokens = slice(j * P, (j + 1) * P)
+            acc_t = psum_t.tile([P, BLOCKS, P], F32)
+            t_sums[j] = acc_t
+            for c in range(BLOCKS):
+                cols = slice(DIRECT + c * P, DIRECT + (c + 1) * P)
+                nc.tensor.matmul_mx(
+                    out=acc_t[:, c, :],
+                    lhsT=w1_words[:, cols].bitcast(FP8X4),
+                    lhsT_scale=w1_scales[:, cols],
+                    rhs=y_words[:, tokens].bitcast(FP8X4),
+                    rhs_scale=y_scales[:, tokens],
+                    start=True,
+                    stop=True,
+                )
+
+        def turned_out(j):
+            h_turned = t_pool.tile([P, BLOCKS, P], F32)
+            t_tiles[j] = h_turned
+            for c in range(BLOCKS):
+                nc.scalar.activation(
+                    out=h_turned[:, c, :],
+                    in_=t_sums[j][:, c, :],
+                    func=ACT.Relu,
+                    bias=bias_turned[:, c : c + 1],
+                    scale=ffn[:, 0:1],
+                )
+
+        def back_turn(j):
             back = psum_back.tile([P, BLOCKS, P], F32)
+            backs[j] = back
             for c in range(BLOCKS):
                 nc.tensor.transpose(back[:, c, :], t_tiles[j][:, c, :], identity[:])
-            h = h_tiles[j]
-            nc.scalar.copy(out=h[:, DIRECT:FF], in_=back[:].rearrange("p c r -> p (c r)"))
+
+        def back_copy(j):
+            h = h_pool.tile([P, FF], F32)
+            h_tiles[j] = h
+            nc.scalar.copy(out=h[:, DIRECT:FF], in_=backs[j][:].rearrange("p c r -> p (c r)"))
             nc.sync.dma_start(out=out_dram[:, j, DIRECT:FF], in_=h[:, DIRECT:FF])
 
-        ctx.enter_context(tc.manual_schedule(engines={mybir.EngineType.PE}))
+        def stage(function, j):
+            if 0 <= j < TILES:
+                function(j)
+
+        ctx.enter_context(tc.manual_schedule(engines={mybir.EngineType.PE, mybir.EngineType.DVE}))
         for step in range(TILES + 4):
-            if step < TILES:
-                quantise_o(step)
-            if 0 <= step - 4 < TILES:
-                turn_back(step - 4)
-            if 0 <= step - 2 < TILES:
-                quantise_y(step - 2)
-            if 0 <= step - 1 < TILES:
-                attention_output(step - 1)
-            if step in (1, 2):
-                for bank in range(2 * (step - 1), min(2 * step, DIRECT // BANK)):
-                    spread_bias(bank)
+            stage(y_turn, step - 2)
+            stage(o_turn, step)
+            stage(back_turn, step - 4)
+            stage(y_copy, step - 2)
+            stage(o_copy, step)
+            stage(back_copy, step - 4)
+            stage(attention_pass, step - 1)
+            stage(direct_out, step - 4)
+            stage(turned_passes, step - 3)
+            stage(turned_out, step - 3)
+            stage(direct_passes, step - 3)
+            stage(attention_add, step - 1)
+            stage(y_quantise, step - 2)
+            stage(o_quantise, step)
+            if step == 1:
+                spread_bias(0)
+                spread_bias(1)
             if step == 2:
+                spread_bias(2)
                 turn_bias()
-            if 0 <= step - 3 < TILES:
-                feed_forward(step - 3)

@@ -274,7 +274,9 @@ def tile_transformerconvblock_pb_kernel(
             if 0 <= j < TILES:
                 function(j)
 
-        ctx.enter_context(tc.manual_schedule(engines={mybir.EngineType.PE, mybir.EngineType.DVE}))
+        ctx.enter_context(
+            tc.manual_schedule(engines={mybir.EngineType.PE, mybir.EngineType.DVE, mybir.EngineType.Activation})
+        )
         for step in range(TILES + 4):
             stage(y_turn, step - 2)
             stage(o_turn, step)
@@ -283,9 +285,9 @@ def tile_transformerconvblock_pb_kernel(
             stage(o_copy, step)
             stage(back_copy, step - 4)
             stage(attention_pass, step - 1)
-            stage(direct_out, step - 4)
             stage(turned_passes, step - 3)
             stage(turned_out, step - 3)
+            stage(direct_out, step - 4)
             stage(direct_passes, step - 3)
             stage(attention_add, step - 1)
             stage(y_quantise, step - 2)

@@ -28,6 +28,8 @@ DIRECT = FF - TURNED
 BLOCKS = TURNED // P
 POOL_BANKS = 2
 LARGEST = 3.0e38
+Y_LAG = 2
+UNITS = 2 * (TILES + Y_LAG)
 QUADRANTS = 4
 
 FLOPS = 2 * TOKENS * K * (CH + FF)
@@ -58,12 +60,9 @@ def tile_transformerconvblock_pb_kernel(
         wo_scales = keep.tile([P, CH], U8, align_bytes=64)
         w1_words = keep.tile([P, FF], U32, align_bytes=64)
         w1_scales = keep.tile([P, FF], U8, align_bytes=64)
-        o_grouped = keep.tile([P, TILES * P * PACK], BF16, align_bytes=64)
-        y_grouped = keep.tile([P, TILES * P * PACK], BF16, align_bytes=64)
-        o_words = keep.tile([P, TOKENS], U32, align_bytes=64)
-        o_scales = keep.tile([P, TOKENS], U8, align_bytes=64)
-        y_words = keep.tile([P, TOKENS], U32, align_bytes=64)
-        y_scales = keep.tile([P, TOKENS], U8, align_bytes=64)
+        grouped = keep.tile([P, UNITS * K], BF16, align_bytes=64)
+        words = keep.tile([P, UNITS * P], U32, align_bytes=64)
+        scales = keep.tile([P, UNITS * P], U8, align_bytes=64)
 
         nc.vector.memset(wo_scales[:].bitcast(I32), 0)
         nc.vector.memset(w1_scales[:].bitcast(I32), 0)
@@ -136,11 +135,19 @@ def tile_transformerconvblock_pb_kernel(
                 nc.tensor.transpose(turned[:, u, :], words[:, u : K // 2 : 2], identity[:])
             return turned
 
-        def quantise(grouped, words, scales, j):
+        def o_unit(j):
+            return 2 * j
+
+        def y_unit(j):
+            return 2 * (j + Y_LAG) + 1
+
+        def quantise(step):
+            first = o_unit(step) if step < TILES else y_unit(step - Y_LAG)
+            last = y_unit(step - Y_LAG) if step >= Y_LAG else o_unit(step)
             nc.vector.quantize_mx(
-                out=words[:, j * P : (j + 1) * P].bitcast(FP8X4),
-                scales=scales[:, j * P : (j + 1) * P],
-                in_=grouped[:, j * K : (j + 1) * K],
+                out=words[:, first * P : (last + 1) * P].bitcast(FP8X4),
+                scales=scales[:, first * P : (last + 1) * P],
+                in_=grouped[:, first * K : (last + 1) * K],
             )
 
         o_turned, y_turned, y_sums, h_sums, t_sums, h_tiles, t_tiles, backs = {}, {}, {}, {}, {}, {}, {}, {}
@@ -150,21 +157,18 @@ def tile_transformerconvblock_pb_kernel(
 
         def o_copy(j):
             nc.scalar.copy(
-                out=o_grouped[:, j * K : (j + 1) * K].bitcast(F32).rearrange("p (r u) -> p r u", u=2),
+                out=grouped[:, o_unit(j) * K : (o_unit(j) + 1) * K].bitcast(F32).rearrange("p (r u) -> p r u", u=2),
                 in_=o_turned[j][:].rearrange("p u r -> p r u"),
             )
 
-        def o_quantise(j):
-            quantise(o_grouped, o_words, o_scales, j)
-
         def attention_pass(j):
-            tokens = slice(j * P, (j + 1) * P)
+            tokens = slice(o_unit(j) * P, (o_unit(j) + 1) * P)
             acc_y = psum_y.tile([P, CH], F32)
             y_sums[j] = acc_y
             nc.tensor.matmul_mx(
                 out=acc_y[:],
-                lhsT=o_words[:, tokens].bitcast(FP8X4),
-                lhsT_scale=o_scales[:, tokens],
+                lhsT=words[:, tokens].bitcast(FP8X4),
+                lhsT_scale=scales[:, tokens],
                 rhs=wo_words[:].bitcast(FP8X4),
                 rhs_scale=wo_scales[:],
                 start=True,
@@ -186,24 +190,21 @@ def tile_transformerconvblock_pb_kernel(
 
         def y_copy(j):
             nc.scalar.activation(
-                out=y_grouped[:, j * K : (j + 1) * K].rearrange("p (r u e) -> p r u e", u=2, e=2),
+                out=grouped[:, y_unit(j) * K : (y_unit(j) + 1) * K].rearrange("p (r u e) -> p r u e", u=2, e=2),
                 in_=y_turned[j][:].bitcast(BF16).rearrange("p u (r e) -> p r u e", e=2),
                 func=ACT.Relu,
             )
 
-        def y_quantise(j):
-            quantise(y_grouped, y_words, y_scales, j)
-
         def direct_passes(j):
-            tokens = slice(j * P, (j + 1) * P)
+            tokens = slice(y_unit(j) * P, (y_unit(j) + 1) * P)
             for bank in range(DIRECT // BANK):
                 cols = slice(bank * BANK, (bank + 1) * BANK)
                 acc_h = psum_h.tile([P, BANK], F32)
                 h_sums[j, bank] = acc_h
                 nc.tensor.matmul_mx(
                     out=acc_h[:],
-                    lhsT=y_words[:, tokens].bitcast(FP8X4),
-                    lhsT_scale=y_scales[:, tokens],
+                    lhsT=words[:, tokens].bitcast(FP8X4),
+                    lhsT_scale=scales[:, tokens],
                     rhs=w1_words[:, cols].bitcast(FP8X4),
                     rhs_scale=w1_scales[:, cols],
                     start=True,
@@ -231,7 +232,7 @@ def tile_transformerconvblock_pb_kernel(
                 nc.sync.dma_start(out=out_dram[:, j, cols], in_=h[:, cols])
 
         def turned_passes(j):
-            tokens = slice(j * P, (j + 1) * P)
+            tokens = slice(y_unit(j) * P, (y_unit(j) + 1) * P)
             acc_t = psum_t.tile([P, BLOCKS, P], F32)
             t_sums[j] = acc_t
             for c in range(BLOCKS):
@@ -240,8 +241,8 @@ def tile_transformerconvblock_pb_kernel(
                     out=acc_t[:, c, :],
                     lhsT=w1_words[:, cols].bitcast(FP8X4),
                     lhsT_scale=w1_scales[:, cols],
-                    rhs=y_words[:, tokens].bitcast(FP8X4),
-                    rhs_scale=y_scales[:, tokens],
+                    rhs=words[:, tokens].bitcast(FP8X4),
+                    rhs_scale=scales[:, tokens],
                     start=True,
                     stop=True,
                 )
@@ -290,8 +291,8 @@ def tile_transformerconvblock_pb_kernel(
             stage(direct_out, step - 4)
             stage(direct_passes, step - 3)
             stage(attention_add, step - 1)
-            stage(y_quantise, step - 2)
-            stage(o_quantise, step)
+            if step < TILES + Y_LAG:
+                quantise(step)
             if step == 1:
                 spread_bias(0)
                 spread_bias(1)

@@ -65,19 +65,23 @@ def tile_transformerconvblock_pb_kernel(
         scales = keep.tile([P, UNITS * P], U8, align_bytes=64)
 
         nc.vector.memset(wo_scales[:].bitcast(I32), 0)
-        nc.vector.memset(w1_scales[:].bitcast(I32), 0)
         bias_row = keep.tile([P, FF], BF16)
         nc.vector.memset(bias_row[:].bitcast(I32), 0)
+        nc.vector.memset(w1_scales[:].bitcast(I32), 0)
         ones = keep.tile([P, P], BF16)
         nc.vector.memset(ones[:], 1.0)
         identity = keep.tile([P, P], F32)
         make_identity(nc, identity[:])
 
+        first = keep.tile([P, 1], F32)
+        nc.gpsimd.memset(first[:], 0.0)
+
         attn_bf16 = keep.tile([P, 1], BF16)
         nc.scalar.dma_start(out=attn_bf16[:], in_=scale_attn.partition_broadcast(P))
-        nc.scalar.dma_start(out=bias_row[0:1, :], in_=ffn1_b.unsqueeze(0))
         ffn_bf16 = keep.tile([P, 1], BF16)
         nc.scalar.dma_start(out=ffn_bf16[:], in_=scale_ffn.partition_broadcast(P))
+        nc.scalar.activation(out=first[:], in_=first[:], func=ACT.Relu)
+        nc.scalar.dma_start(out=bias_row[0:1, :], in_=ffn1_b.unsqueeze(0))
 
         def load_tokens(part):
             tiles = slice(part * LOAD, (part + 1) * LOAD)
@@ -101,18 +105,22 @@ def tile_transformerconvblock_pb_kernel(
         load_tokens(2)
         load_tokens(3)
 
-        attn = keep.tile([P, 1], F32)
-        nc.vector.tensor_copy(out=attn[:], in_=attn_bf16[:])
         ffn = keep.tile([P, 1], F32)
-        nc.vector.tensor_copy(out=ffn[:], in_=ffn_bf16[:])
+        nc.scalar.copy(out=ffn[:], in_=ffn_bf16[:])
 
         bias_all = keep.tile([P, DIRECT], F32)
 
+        spreads = {}
+
         def spread_bias(bank):
             cols = slice(bank * BANK, (bank + 1) * BANK)
-            spread = psum_h.tile([P, BANK], F32, tag="acc_h")
+            spread = psum_h.tile([P, BANK], F32, name="acc_h")
+            spreads[bank] = spread
             nc.tensor.matmul(spread[:], lhsT=ones[:], rhs=bias_row[:, cols], start=True, stop=True)
-            nc.vector.tensor_scalar_mul(out=bias_all[:, cols], in0=spread[:], scalar1=ffn[:, 0:1])
+
+        def spread_out(bank):
+            cols = slice(bank * BANK, (bank + 1) * BANK)
+            nc.scalar.activation(out=bias_all[:, cols], in_=spreads[bank][:], func=ACT.Copy, scale=ffn[:, 0:1])
 
         bias_turned = keep.tile([P, BLOCKS], F32)
 
@@ -126,10 +134,10 @@ def tile_transformerconvblock_pb_kernel(
                     start=True,
                     stop=True,
                 )
-            nc.vector.tensor_scalar_mul(out=bias_turned[:], in0=column[:], scalar1=ffn[:, 0:1])
+            nc.scalar.activation(out=bias_turned[:], in_=column[:], func=ACT.Copy, scale=ffn[:, 0:1])
 
-        def turn(rows, j):
-            turned = psum_turn.tile([P, 2, P], F32)
+        def turn(rows, j, pool=psum_turn, name="turned"):
+            turned = pool.tile([P, 2, P], F32, name=name)
             words = rows[:, j, :].bitcast(F32)
             for u in range(2):
                 nc.tensor.transpose(turned[:, u, :], words[:, u : K // 2 : 2], identity[:])
@@ -140,6 +148,13 @@ def tile_transformerconvblock_pb_kernel(
 
         def y_unit(j):
             return 2 * (j + Y_LAG) + 1
+
+        def quantise_unit(unit):
+            nc.vector.quantize_mx(
+                out=words[:, unit * P : (unit + 1) * P].bitcast(FP8X4),
+                scales=scales[:, unit * P : (unit + 1) * P],
+                in_=grouped[:, unit * K : (unit + 1) * K],
+            )
 
         def quantise(step):
             first = o_unit(step) if step < TILES else y_unit(step - Y_LAG)
@@ -152,8 +167,8 @@ def tile_transformerconvblock_pb_kernel(
 
         o_turned, y_turned, y_sums, h_sums, t_sums, h_tiles, t_tiles, backs = {}, {}, {}, {}, {}, {}, {}, {}
 
-        def o_turn(j):
-            o_turned[j] = turn(o_rows, j)
+        def o_turn(j, *where):
+            o_turned[j] = turn(o_rows, j, *where)
 
         def o_copy(j):
             nc.scalar.copy(
@@ -163,7 +178,10 @@ def tile_transformerconvblock_pb_kernel(
 
         def attention_pass(j):
             tokens = slice(o_unit(j) * P, (o_unit(j) + 1) * P)
-            acc_y = psum_y.tile([P, CH], F32)
+            if j in (1, 3):
+                acc_y = psum_t.tile([P, BLOCKS, P], F32, name="acc_t")[:].rearrange("p c r -> p (c r)")
+            else:
+                acc_y = psum_y.tile([P, CH], F32)
             y_sums[j] = acc_y
             nc.tensor.matmul_mx(
                 out=acc_y[:],
@@ -179,7 +197,7 @@ def tile_transformerconvblock_pb_kernel(
             nc.vector.scalar_tensor_tensor(
                 out=y_rows[:, j, :],
                 in0=y_sums[j][:],
-                scalar=attn[:, 0:1],
+                scalar=attn_bf16[:, 0:1],
                 in1=xn_rows[:, j, :],
                 op0=ALU.mult,
                 op1=ALU.add,
@@ -195,21 +213,24 @@ def tile_transformerconvblock_pb_kernel(
                 func=ACT.Relu,
             )
 
-        def direct_passes(j):
+        def direct_pass(j, bank):
             tokens = slice(y_unit(j) * P, (y_unit(j) + 1) * P)
+            cols = slice(bank * BANK, (bank + 1) * BANK)
+            acc_h = psum_h.tile([P, BANK], F32)
+            h_sums[j, bank] = acc_h
+            nc.tensor.matmul_mx(
+                out=acc_h[:],
+                lhsT=words[:, tokens].bitcast(FP8X4),
+                lhsT_scale=scales[:, tokens],
+                rhs=w1_words[:, cols].bitcast(FP8X4),
+                rhs_scale=w1_scales[:, cols],
+                start=True,
+                stop=True,
+            )
+
+        def direct_passes(j):
             for bank in range(DIRECT // BANK):
-                cols = slice(bank * BANK, (bank + 1) * BANK)
-                acc_h = psum_h.tile([P, BANK], F32)
-                h_sums[j, bank] = acc_h
-                nc.tensor.matmul_mx(
-                    out=acc_h[:],
-                    lhsT=words[:, tokens].bitcast(FP8X4),
-                    lhsT_scale=scales[:, tokens],
-                    rhs=w1_words[:, cols].bitcast(FP8X4),
-                    rhs_scale=w1_scales[:, cols],
-                    start=True,
-                    stop=True,
-                )
+                direct_pass(j, bank)
 
         def direct_out(j):
             h = h_tiles[j]
@@ -278,24 +299,57 @@ def tile_transformerconvblock_pb_kernel(
         ctx.enter_context(
             tc.manual_schedule(engines={mybir.EngineType.PE, mybir.EngineType.DVE, mybir.EngineType.Activation})
         )
-        for step in range(TILES + 4):
+        for j in range(2):
+            o_turn(j)
+            o_copy(j)
+            quantise_unit(o_unit(j))
+        spread_bias(0)
+        spread_out(0)
+        attention_pass(0)
+        attention_pass(1)
+        o_turn(2, psum_back, "back")
+        o_copy(2)
+        attention_add(0)
+        attention_add(1)
+        o_turn(3, psum_h, "acc_h")
+        o_copy(3)
+        y_turn(0)
+        y_copy(0)
+        y_turn(1)
+        y_copy(1)
+        quantise_unit(o_unit(2))
+        quantise_unit(o_unit(3))
+        spread_bias(1)
+        attention_pass(2)
+        attention_pass(3)
+        spread_out(1)
+        quantise_unit(y_unit(0))
+        spread_bias(2)
+        attention_add(2)
+        quantise_unit(y_unit(1))
+        direct_pass(0, 0)
+        attention_add(3)
+        spread_out(2)
+        direct_pass(0, 1)
+        turn_bias()
+        direct_pass(0, 2)
+        turned_passes(0)
+        turned_out(0)
+
+        for step in range(4, TILES + 4):
             stage(y_turn, step - 2)
             stage(o_turn, step)
             stage(back_turn, step - 4)
             stage(y_copy, step - 2)
             stage(o_copy, step)
             stage(back_copy, step - 4)
-            stage(attention_pass, step - 1)
+            if step > 4:
+                stage(attention_pass, step - 1)
             stage(turned_passes, step - 3)
             stage(turned_out, step - 3)
             stage(direct_out, step - 4)
             stage(direct_passes, step - 3)
-            stage(attention_add, step - 1)
+            if step > 4:
+                stage(attention_add, step - 1)
             if step < TILES + Y_LAG:
                 quantise(step)
-            if step == 1:
-                spread_bias(0)
-                spread_bias(1)
-            if step == 2:
-                spread_bias(2)
-                turn_bias()

@@ -106,7 +106,6 @@ def tile_transformerconvblock_pb_kernel(
         load_tokens(3)
 
         ffn = keep.tile([P, 1], F32)
-        nc.scalar.copy(out=ffn[:], in_=ffn_bf16[:])
 
         bias_all = keep.tile([P, DIRECT], F32)
 
@@ -136,8 +135,9 @@ def tile_transformerconvblock_pb_kernel(
                 )
             nc.scalar.activation(out=bias_turned[:], in_=column[:], func=ACT.Copy, scale=ffn[:, 0:1])
 
-        def turn(rows, j, pool=psum_turn, name="turned"):
-            turned = pool.tile([P, 2, P], F32, name=name)
+        def turn(rows, j, turned=None):
+            if turned is None:
+                turned = psum_turn.tile([P, 2, P], F32)
             words = rows[:, j, :].bitcast(F32)
             for u in range(2):
                 nc.tensor.transpose(turned[:, u, :], words[:, u : K // 2 : 2], identity[:])
@@ -232,25 +232,27 @@ def tile_transformerconvblock_pb_kernel(
             for bank in range(DIRECT // BANK):
                 direct_pass(j, bank)
 
-        def direct_out(j):
+        def direct_out(j, bank):
+            if bank == 0:
+                h = h_pool.tile([P, FF], F32)
+                h_tiles[j] = h
             h = h_tiles[j]
-            for bank in range(DIRECT // BANK):
-                cols = slice(bank * BANK, (bank + 1) * BANK)
-                nc.vector.scalar_tensor_tensor(
-                    out=h[:, cols],
-                    in0=h_sums[j, bank][:],
-                    scalar=ffn[:, 0:1],
-                    in1=bias_all[:, cols],
-                    op0=ALU.mult,
-                    op1=ALU.add,
+            cols = slice(bank * BANK, (bank + 1) * BANK)
+            nc.vector.scalar_tensor_tensor(
+                out=h[:, cols],
+                in0=h_sums[j, bank][:],
+                scalar=ffn[:, 0:1],
+                in1=bias_all[:, cols],
+                op0=ALU.mult,
+                op1=ALU.add,
+            )
+            if bank < POOL_BANKS or j == 0:
+                nc.gpsimd.tensor_scalar(
+                    out=h[:, cols], in0=h[:, cols], scalar1=LARGEST, scalar2=0.0, op0=ALU.min, op1=ALU.max
                 )
-                if bank < POOL_BANKS:
-                    nc.gpsimd.tensor_scalar(
-                        out=h[:, cols], in0=h[:, cols], scalar1=LARGEST, scalar2=0.0, op0=ALU.min, op1=ALU.max
-                    )
-                else:
-                    nc.scalar.activation(out=h[:, cols], in_=h[:, cols], func=ACT.Relu)
-                nc.sync.dma_start(out=out_dram[:, j, cols], in_=h[:, cols])
+            else:
+                nc.scalar.activation(out=h[:, cols], in_=h[:, cols], func=ACT.Relu)
+            nc.sync.dma_start(out=out_dram[:, j, cols], in_=h[:, cols])
 
         def turned_passes(j):
             tokens = slice(y_unit(j) * P, (y_unit(j) + 1) * P)
@@ -287,14 +289,13 @@ def tile_transformerconvblock_pb_kernel(
                 nc.tensor.transpose(back[:, c, :], t_tiles[j][:, c, :], identity[:])
 
         def back_copy(j):
-            h = h_pool.tile([P, FF], F32)
-            h_tiles[j] = h
+            h = h_tiles[j]
             nc.scalar.copy(out=h[:, DIRECT:FF], in_=backs[j][:].rearrange("p c r -> p (c r)"))
             nc.sync.dma_start(out=out_dram[:, j, DIRECT:FF], in_=h[:, DIRECT:FF])
 
-        def stage(function, j):
+        def stage(function, j, *rest):
             if 0 <= j < TILES:
-                function(j)
+                function(j, *rest)
 
         ctx.enter_context(
             tc.manual_schedule(engines={mybir.EngineType.PE, mybir.EngineType.DVE, mybir.EngineType.Activation})
@@ -303,33 +304,34 @@ def tile_transformerconvblock_pb_kernel(
             o_turn(j)
             o_copy(j)
             quantise_unit(o_unit(j))
-        spread_bias(0)
-        spread_out(0)
         attention_pass(0)
         attention_pass(1)
-        o_turn(2, psum_back, "back")
-        o_copy(2)
+        spread_bias(0)
         attention_add(0)
         attention_add(1)
-        o_turn(3, psum_h, "acc_h")
-        o_copy(3)
+        pair = psum_back.tile([P, 4, P], F32, name="back")
+        for j in (2, 3):
+            o_turn(j, pair[:, 2 * j - 4 : 2 * j - 2, :])
+            o_copy(j)
+            quantise_unit(o_unit(j))
         y_turn(0)
         y_copy(0)
+        nc.scalar.copy(out=ffn[:], in_=ffn_bf16[:])
+        spread_out(0)
         y_turn(1)
         y_copy(1)
-        quantise_unit(o_unit(2))
-        quantise_unit(o_unit(3))
-        spread_bias(1)
         attention_pass(2)
-        attention_pass(3)
-        spread_out(1)
         quantise_unit(y_unit(0))
-        spread_bias(2)
+        attention_pass(3)
         attention_add(2)
-        quantise_unit(y_unit(1))
         direct_pass(0, 0)
-        attention_add(3)
+        spread_bias(1)
+        spread_out(1)
+        quantise_unit(y_unit(1))
+        direct_out(0, 0)
+        spread_bias(2)
         spread_out(2)
+        attention_add(3)
         direct_pass(0, 1)
         turn_bias()
         direct_pass(0, 2)
@@ -347,9 +349,13 @@ def tile_transformerconvblock_pb_kernel(
                 stage(attention_pass, step - 1)
             stage(turned_passes, step - 3)
             stage(turned_out, step - 3)
-            stage(direct_out, step - 4)
-            stage(direct_passes, step - 3)
+            stage(direct_pass, step - 3, 0)
+            stage(direct_out, step - 4, 1)
+            stage(direct_pass, step - 3, 1)
+            stage(direct_out, step - 4, 2)
+            stage(direct_pass, step - 3, 2)
             if step > 4:
                 stage(attention_add, step - 1)
+            stage(direct_out, step - 3, 0)
             if step < TILES + Y_LAG:
                 quantise(step)

@@ -19,7 +19,6 @@ TOKENS = 1024
 TILES = TOKENS // P
 PAIR = 1
 PAIRS = TILES // PAIR
-LOAD = 2
 CH = 512
 FF = 2048
 BANK = 512
@@ -79,31 +78,36 @@ def tile_transformerconvblock_pb_kernel(
         attn_bf16 = keep.tile([P, 1], BF16)
         nc.scalar.dma_start(out=attn_bf16[:], in_=scale_attn.partition_broadcast(P))
         ffn_bf16 = keep.tile([P, 1], BF16)
-        nc.scalar.dma_start(out=ffn_bf16[:], in_=scale_ffn.partition_broadcast(P))
+        nc.gpsimd.dma_start(out=ffn_bf16[:], in_=scale_ffn.partition_broadcast(P))
         nc.scalar.activation(out=first[:], in_=first[:], func=ACT.Relu)
         nc.scalar.dma_start(out=bias_row[0:1, :], in_=ffn1_b.unsqueeze(0))
 
-        def load_tokens(part):
-            tiles = slice(part * LOAD, (part + 1) * LOAD)
-            nc.sync.dma_start(out=o_rows[:, tiles, :], in_=o_dram[:, tiles, :])
-            nc.sync.dma_start(out=xn_rows[:, tiles, :], in_=xn_dram[:, tiles, :])
+        def load_rows(rows, dram, first, count):
+            tiles = slice(first, first + count)
+            nc.sync.dma_start(out=rows[:, tiles, :], in_=dram[:, tiles, :])
 
-        def load_weight(words, scales, words_dram, scales_dram):
+        def load_words(words, words_dram):
             nc.sync.dma_start(
                 out=words[:].bitcast(I32), in_=words_dram.rearrange("g p n t -> (g p) (n t)").bitcast(I32)
             )
+
+        def load_scales(scales, scales_dram):
             for q in range(QUADRANTS):
                 nc.sync.dma_start(
                     out=scales[32 * q : 32 * q + 4, :].bitcast(I32),
                     in_=scales_dram[0, 4 * q : 4 * q + 4, :].bitcast(I32),
                 )
 
-        load_tokens(0)
-        load_weight(wo_words, wo_scales, W_O_words, W_O_scales)
-        load_tokens(1)
-        load_weight(w1_words, w1_scales, ffn1_w_words, ffn1_w_scales)
-        load_tokens(2)
-        load_tokens(3)
+        load_rows(o_rows, o_dram, 0, 2)
+        load_scales(wo_scales, W_O_scales)
+        load_words(wo_words, W_O_words)
+        load_rows(xn_rows, xn_dram, 0, 2)
+        load_rows(o_rows, o_dram, 2, 2)
+        load_rows(xn_rows, xn_dram, 2, 2)
+        load_scales(w1_scales, ffn1_w_scales)
+        load_words(w1_words, ffn1_w_words)
+        load_rows(o_rows, o_dram, 4, 4)
+        load_rows(xn_rows, xn_dram, 4, 4)
 
         ffn = keep.tile([P, 1], F32)
 
@@ -111,9 +115,8 @@ def tile_transformerconvblock_pb_kernel(
 
         spreads = {}
 
-        def spread_bias(bank):
+        def spread_bias(bank, spread):
             cols = slice(bank * BANK, (bank + 1) * BANK)
-            spread = psum_h.tile([P, BANK], F32, name="acc_h")
             spreads[bank] = spread
             nc.tensor.matmul(spread[:], lhsT=ones[:], rhs=bias_row[:, cols], start=True, stop=True)
 
@@ -124,7 +127,7 @@ def tile_transformerconvblock_pb_kernel(
         bias_turned = keep.tile([P, BLOCKS], F32)
 
         def turn_bias():
-            column = psum_back.tile([P, BLOCKS], F32, tag="back")
+            column = psum_turn.tile([P, BLOCKS], F32, name="turned")
             for c in range(BLOCKS):
                 nc.tensor.matmul(
                     column[:, c : c + 1],
@@ -306,56 +309,72 @@ def tile_transformerconvblock_pb_kernel(
             quantise_unit(o_unit(j))
         attention_pass(0)
         attention_pass(1)
-        spread_bias(0)
+        o_turn(2, psum_h.tile([P, 2, P], F32, name="acc_h"))
+        o_copy(2)
         attention_add(0)
         attention_add(1)
-        pair = psum_back.tile([P, 4, P], F32, name="back")
-        for j in (2, 3):
-            o_turn(j, pair[:, 2 * j - 4 : 2 * j - 2, :])
-            o_copy(j)
-            quantise_unit(o_unit(j))
+        o_turn(3, psum_back.tile([P, 2, P], F32, name="back"))
+        o_copy(3)
         y_turn(0)
         y_copy(0)
-        nc.scalar.copy(out=ffn[:], in_=ffn_bf16[:])
-        spread_out(0)
         y_turn(1)
         y_copy(1)
+        quantise_unit(o_unit(2))
+        quantise_unit(o_unit(3))
+        spread_bias(0, psum_h.tile([P, BANK], F32, name="acc_h"))
         attention_pass(2)
+        nc.scalar.copy(out=ffn[:], in_=ffn_bf16[:])
+        spread_out(0)
+        spread_bias(1, psum_h.tile([P, BANK], F32, name="acc_h"))
+        spread_out(1)
         quantise_unit(y_unit(0))
+        direct_pass(0, 0)
         attention_pass(3)
         attention_add(2)
-        direct_pass(0, 0)
-        spread_bias(1)
-        spread_out(1)
+        spread_bias(2, psum_back.tile([P, BANK], F32, name="back"))
+        spread_out(2)
+        turn_bias()
         quantise_unit(y_unit(1))
         direct_out(0, 0)
-        spread_bias(2)
-        spread_out(2)
         attention_add(3)
         direct_pass(0, 1)
-        turn_bias()
         direct_pass(0, 2)
+        y_turn(2)
+        y_copy(2)
+        o_turn(4)
+        o_copy(4)
         turned_passes(0)
         turned_out(0)
+        direct_pass(1, 0)
+        direct_out(0, 1)
+        direct_pass(1, 1)
+        direct_out(0, 2)
+        direct_out(1, 0)
+        quantise(4)
+        back_turn(0)
+        back_copy(0)
+        direct_pass(1, 2)
+        turned_passes(1)
+        attention_pass(4)
+        turned_out(1)
 
-        for step in range(4, TILES + 4):
+        for step in range(5, TILES + 4):
             stage(y_turn, step - 2)
             stage(o_turn, step)
             stage(back_turn, step - 4)
             stage(y_copy, step - 2)
             stage(o_copy, step)
             stage(back_copy, step - 4)
-            if step > 4:
+            if step > 5:
                 stage(attention_pass, step - 1)
+            stage(direct_pass, step - 3, 0)
             stage(turned_passes, step - 3)
             stage(turned_out, step - 3)
-            stage(direct_pass, step - 3, 0)
             stage(direct_out, step - 4, 1)
             stage(direct_pass, step - 3, 1)
             stage(direct_out, step - 4, 2)
             stage(direct_pass, step - 3, 2)
-            if step > 4:
-                stage(attention_add, step - 1)
+            stage(attention_add, step - 1)
             stage(direct_out, step - 3, 0)
             if step < TILES + Y_LAG:
                 quantise(step)

@@ -29,6 +29,7 @@ POOL_BANKS = 2
 LARGEST = 3.0e38
 Y_LAG = 2
 UNITS = 2 * (TILES + Y_LAG)
+ATTN, FFN, FACTORS = 0, 32, 64
 QUADRANTS = 4
 
 FLOPS = 2 * TOKENS * K * (CH + FF)
@@ -63,6 +64,8 @@ def tile_transformerconvblock_pb_kernel(
         words = keep.tile([P, UNITS * P], U32, align_bytes=64)
         scales = keep.tile([P, UNITS * P], U8, align_bytes=64)
 
+        factor_row = keep.tile([P, FACTORS], BF16)
+        nc.vector.memset(factor_row[:].bitcast(I32), 0)
         nc.vector.memset(wo_scales[:].bitcast(I32), 0)
         bias_row = keep.tile([P, FF], BF16)
         nc.vector.memset(bias_row[:].bitcast(I32), 0)
@@ -75,11 +78,9 @@ def tile_transformerconvblock_pb_kernel(
         first = keep.tile([P, 1], F32)
         nc.gpsimd.memset(first[:], 0.0)
 
-        attn_bf16 = keep.tile([P, 1], BF16)
-        nc.scalar.dma_start(out=attn_bf16[:], in_=scale_attn.partition_broadcast(P))
-        ffn_bf16 = keep.tile([P, 1], BF16)
-        nc.gpsimd.dma_start(out=ffn_bf16[:], in_=scale_ffn.partition_broadcast(P))
+        nc.scalar.dma_start(out=factor_row[0:1, ATTN : ATTN + 1], in_=scale_attn.unsqueeze(0))
         nc.scalar.activation(out=first[:], in_=first[:], func=ACT.Relu)
+        nc.scalar.dma_start(out=factor_row[0:1, FFN : FFN + 1], in_=scale_ffn.unsqueeze(0))
         nc.scalar.dma_start(out=bias_row[0:1, :], in_=ffn1_b.unsqueeze(0))
 
         def load_rows(rows, dram, first, count):
@@ -103,13 +104,22 @@ def tile_transformerconvblock_pb_kernel(
         load_words(wo_words, W_O_words)
         load_rows(xn_rows, xn_dram, 0, 2)
         load_rows(o_rows, o_dram, 2, 2)
+        load_words(w1_words, ffn1_w_words)
         load_rows(xn_rows, xn_dram, 2, 2)
         load_scales(w1_scales, ffn1_w_scales)
-        load_words(w1_words, ffn1_w_words)
         load_rows(o_rows, o_dram, 4, 4)
         load_rows(xn_rows, xn_dram, 4, 4)
 
-        ffn = keep.tile([P, 1], F32)
+        factors = keep.tile([P, FACTORS], F32)
+
+        def spread_factor(first):
+            cols = slice(first, first + 32)
+            spread = psum_back.tile([P, 32], F32, name="back")
+            nc.tensor.matmul(spread[:], lhsT=ones[:], rhs=factor_row[:, cols], start=True, stop=True)
+            nc.scalar.copy(out=factors[:, cols], in_=spread[:])
+
+        attn = factors[:, ATTN : ATTN + 1]
+        ffn = factors[:, FFN : FFN + 1]
 
         bias_all = keep.tile([P, DIRECT], F32)
 
@@ -122,7 +132,7 @@ def tile_transformerconvblock_pb_kernel(
 
         def spread_out(bank):
             cols = slice(bank * BANK, (bank + 1) * BANK)
-            nc.scalar.activation(out=bias_all[:, cols], in_=spreads[bank][:], func=ACT.Copy, scale=ffn[:, 0:1])
+            nc.scalar.activation(out=bias_all[:, cols], in_=spreads[bank][:], func=ACT.Copy, scale=ffn)
 
         bias_turned = keep.tile([P, BLOCKS], F32)
 
@@ -136,7 +146,7 @@ def tile_transformerconvblock_pb_kernel(
                     start=True,
                     stop=True,
                 )
-            nc.scalar.activation(out=bias_turned[:], in_=column[:], func=ACT.Copy, scale=ffn[:, 0:1])
+            nc.scalar.activation(out=bias_turned[:], in_=column[:], func=ACT.Copy, scale=ffn)
 
         def turn(rows, j, turned=None):
             if turned is None:
@@ -200,7 +210,7 @@ def tile_transformerconvblock_pb_kernel(
             nc.vector.scalar_tensor_tensor(
                 out=y_rows[:, j, :],
                 in0=y_sums[j][:],
-                scalar=attn_bf16[:, 0:1],
+                scalar=attn,
                 in1=xn_rows[:, j, :],
                 op0=ALU.mult,
                 op1=ALU.add,
@@ -244,7 +254,7 @@ def tile_transformerconvblock_pb_kernel(
             nc.vector.scalar_tensor_tensor(
                 out=h[:, cols],
                 in0=h_sums[j, bank][:],
-                scalar=ffn[:, 0:1],
+                scalar=ffn,
                 in1=bias_all[:, cols],
                 op0=ALU.mult,
                 op1=ALU.add,
@@ -282,7 +292,7 @@ def tile_transformerconvblock_pb_kernel(
                     in_=t_sums[j][:, c, :],
                     func=ACT.Relu,
                     bias=bias_turned[:, c : c + 1],
-                    scale=ffn[:, 0:1],
+                    scale=ffn,
                 )
 
         def back_turn(j):
@@ -307,6 +317,7 @@ def tile_transformerconvblock_pb_kernel(
             o_turn(j)
             o_copy(j)
             quantise_unit(o_unit(j))
+        spread_factor(ATTN)
         attention_pass(0)
         attention_pass(1)
         o_turn(2, psum_h.tile([P, 2, P], F32, name="acc_h"))
@@ -321,9 +332,9 @@ def tile_transformerconvblock_pb_kernel(
         y_copy(1)
         quantise_unit(o_unit(2))
         quantise_unit(o_unit(3))
+        spread_factor(FFN)
         spread_bias(0, psum_h.tile([P, BANK], F32, name="acc_h"))
         attention_pass(2)
-        nc.scalar.copy(out=ffn[:], in_=ffn_bf16[:])
         spread_out(0)
         spread_bias(1, psum_h.tile([P, BANK], F32, name="acc_h"))
         spread_out(1)

@@ -80,8 +80,6 @@ def tile_transformerconvblock_pb_kernel(
 
         nc.scalar.dma_start(out=factor_row[0:1, ATTN : ATTN + 1], in_=scale_attn.unsqueeze(0))
         nc.scalar.activation(out=first[:], in_=first[:], func=ACT.Relu)
-        nc.scalar.dma_start(out=factor_row[0:1, FFN : FFN + 1], in_=scale_ffn.unsqueeze(0))
-        nc.scalar.dma_start(out=bias_row[0:1, :], in_=ffn1_b.unsqueeze(0))
 
         def load_rows(rows, dram, first, count):
             tiles = slice(first, first + count)
@@ -103,12 +101,15 @@ def tile_transformerconvblock_pb_kernel(
         load_scales(wo_scales, W_O_scales)
         load_words(wo_words, W_O_words)
         load_rows(xn_rows, xn_dram, 0, 2)
+        nc.sync.dma_start(out=factor_row[0:1, FFN : FFN + 1], in_=scale_ffn.unsqueeze(0))
+        nc.sync.dma_start(out=bias_row[0:1, :], in_=ffn1_b.unsqueeze(0))
         load_rows(o_rows, o_dram, 2, 2)
-        load_words(w1_words, ffn1_w_words)
         load_rows(xn_rows, xn_dram, 2, 2)
+        load_words(w1_words, ffn1_w_words)
         load_scales(w1_scales, ffn1_w_scales)
-        load_rows(o_rows, o_dram, 4, 4)
-        load_rows(xn_rows, xn_dram, 4, 4)
+        for first_tile in range(4, TILES, 2):
+            load_rows(o_rows, o_dram, first_tile, 2)
+            load_rows(xn_rows, xn_dram, first_tile, 2)
 
         factors = keep.tile([P, FACTORS], F32)
 
@@ -245,11 +246,14 @@ def tile_transformerconvblock_pb_kernel(
             for bank in range(DIRECT // BANK):
                 direct_pass(j, bank)
 
-        def direct_out(j, bank):
-            if bank == 0:
+        def rows_of_h(j):
+            if j not in h_tiles:
                 h = h_pool.tile([P, FF], F32)
                 h_tiles[j] = h
-            h = h_tiles[j]
+            return h_tiles[j]
+
+        def direct_out(j, bank):
+            h = rows_of_h(j)
             cols = slice(bank * BANK, (bank + 1) * BANK)
             nc.vector.scalar_tensor_tensor(
                 out=h[:, cols],
@@ -302,7 +306,7 @@ def tile_transformerconvblock_pb_kernel(
                 nc.tensor.transpose(back[:, c, :], t_tiles[j][:, c, :], identity[:])
 
         def back_copy(j):
-            h = h_tiles[j]
+            h = rows_of_h(j)
             nc.scalar.copy(out=h[:, DIRECT:FF], in_=backs[j][:].rearrange("p c r -> p (c r)"))
             nc.sync.dma_start(out=out_dram[:, j, DIRECT:FF], in_=h[:, DIRECT:FF])
 
@@ -360,7 +364,6 @@ def tile_transformerconvblock_pb_kernel(
         direct_out(0, 1)
         direct_pass(1, 1)
         direct_out(0, 2)
-        direct_out(1, 0)
         quantise(4)
         back_turn(0)
         back_copy(0)
@@ -378,14 +381,12 @@ def tile_transformerconvblock_pb_kernel(
             stage(back_copy, step - 4)
             if step > 5:
                 stage(attention_pass, step - 1)
-            stage(direct_pass, step - 3, 0)
             stage(turned_passes, step - 3)
             stage(turned_out, step - 3)
-            stage(direct_out, step - 4, 1)
-            stage(direct_pass, step - 3, 1)
-            stage(direct_out, step - 4, 2)
-            stage(direct_pass, step - 3, 2)
+            for bank in range(DIRECT // BANK):
+                stage(direct_out, step - 4, bank)
+            for bank in range(DIRECT // BANK):
+                stage(direct_pass, step - 3, bank)
             stage(attention_add, step - 1)
-            stage(direct_out, step - 3, 0)
             if step < TILES + Y_LAG:
                 quantise(step)

@@ -246,6 +246,9 @@ def tile_transformerconvblock_pb_kernel(
             for bank in range(DIRECT // BANK):
                 direct_pass(j, bank)
 
+        def store(j, cols):
+            nc.sync.dma_start(out=out_dram[:, j, cols], in_=h_tiles[j][:, cols])
+
         def rows_of_h(j):
             if j not in h_tiles:
                 h = h_pool.tile([P, FF], F32)
@@ -269,7 +272,11 @@ def tile_transformerconvblock_pb_kernel(
                 )
             else:
                 nc.scalar.activation(out=h[:, cols], in_=h[:, cols], func=ACT.Relu)
-            nc.sync.dma_start(out=out_dram[:, j, cols], in_=h[:, cols])
+            if j > 0:
+                if bank == 1:
+                    store(j, slice(0, 2 * BANK))
+            else:
+                store(j, cols)
 
         def turned_passes(j):
             tokens = slice(y_unit(j) * P, (y_unit(j) + 1) * P)
@@ -308,7 +315,8 @@ def tile_transformerconvblock_pb_kernel(
         def back_copy(j):
             h = rows_of_h(j)
             nc.scalar.copy(out=h[:, DIRECT:FF], in_=backs[j][:].rearrange("p c r -> p (c r)"))
-            nc.sync.dma_start(out=out_dram[:, j, DIRECT:FF], in_=h[:, DIRECT:FF])
+            if j == 0:
+                store(j, slice(DIRECT, FF))
 
         def stage(function, j, *rest):
             if 0 <= j < TILES:
@@ -385,6 +393,9 @@ def tile_transformerconvblock_pb_kernel(
             stage(turned_out, step - 3)
             for bank in range(DIRECT // BANK):
                 stage(direct_out, step - 4, bank)
+            j = step - 4
+            if 0 < j < TILES:
+                store(j, slice(2 * BANK, FF))
             for bank in range(DIRECT // BANK):
                 stage(direct_pass, step - 3, bank)
             stage(attention_add, step - 1)

from contextlib import ExitStack

import concourse.mybir as mybir
from concourse.masks import make_identity

F32 = mybir.dt.float32
BF16 = mybir.dt.bfloat16
I32 = mybir.dt.int32
U32 = mybir.dt.uint32
U8 = mybir.dt.uint8
FP8X4 = mybir.dt.float8_e4m3fn_x4
ALU = mybir.AluOpType
ACT = mybir.ActivationFunctionType

P = 128
PACK = 4
K = P * PACK
TOKENS = 1024
TILES = TOKENS // P
PAIR = 1
PAIRS = TILES // PAIR
CH = 512
FF = 2048
BANK = 512
TURNED = 512
DIRECT = FF - TURNED
BLOCKS = TURNED // P
POOL_BANKS = 2
LARGEST = 3.0e38
Y_LAG = 2
UNITS = 2 * (TILES + Y_LAG)
ATTN, FFN, FACTORS = 0, 32, 64
QUADRANTS = 4

FLOPS = 2 * TOKENS * K * (CH + FF)


def tile_transformerconvblock_pb_kernel(
    tc, o, xn, W_O_words, W_O_scales, scale_attn, ffn1_w_words, ffn1_w_scales, ffn1_b, scale_ffn, out
):
    nc = tc.nc
    o_dram = o.flatten_outer_dims().rearrange("(p j) k -> p j k", j=TILES)
    xn_dram = xn.flatten_outer_dims().rearrange("(p j) c -> p j c", j=TILES)
    out_dram = out.flatten_outer_dims().rearrange("(p j) f -> p j f", j=TILES)

    with ExitStack() as ctx:
        keep = ctx.enter_context(tc.tile_pool(name="keep", bufs=1))
        h_pool = ctx.enter_context(tc.tile_pool(name="h_pool", bufs=TILES))
        t_pool = ctx.enter_context(tc.tile_pool(name="t_pool", bufs=3))
        psum_turn = ctx.enter_context(tc.psum_pool(name="psum_turn", bufs=2))
        psum_y = ctx.enter_context(tc.psum_pool(name="psum_y", bufs=1))
        psum_h = ctx.enter_context(tc.psum_pool(name="psum_h", bufs=3))
        psum_t = ctx.enter_context(tc.psum_pool(name="psum_t", bufs=1))
        psum_back = ctx.enter_context(tc.psum_pool(name="psum_back", bufs=1))

        o_rows = keep.tile([P, TILES, K], BF16)
        xn_rows = keep.tile([P, TILES, CH], BF16)
        y_rows = keep.tile([P, TILES, CH], BF16)
        wo_words = keep.tile([P, CH], U32, align_bytes=64)
        wo_scales = keep.tile([P, CH], U8, align_bytes=64)
        w1_words = keep.tile([P, FF], U32, align_bytes=64)
        w1_scales = keep.tile([P, FF], U8, align_bytes=64)
        grouped = keep.tile([P, UNITS * K], BF16, align_bytes=64)
        words = keep.tile([P, UNITS * P], U32, align_bytes=64)
        scales = keep.tile([P, UNITS * P], U8, align_bytes=64)

        factor_row = keep.tile([P, FACTORS], BF16)
        nc.vector.memset(factor_row[:].bitcast(I32), 0)
        nc.vector.memset(wo_scales[:].bitcast(I32), 0)
        bias_row = keep.tile([P, FF], BF16)
        nc.vector.memset(bias_row[:].bitcast(I32), 0)
        nc.vector.memset(w1_scales[:].bitcast(I32), 0)
        ones = keep.tile([P, P], BF16)
        nc.vector.memset(ones[:], 1.0)
        identity = keep.tile([P, P], F32)
        make_identity(nc, identity[:])

        first = keep.tile([P, 1], F32)
        nc.gpsimd.memset(first[:], 0.0)

        nc.scalar.dma_start(out=factor_row[0:1, ATTN : ATTN + 1], in_=scale_attn.unsqueeze(0))
        nc.scalar.activation(out=first[:], in_=first[:], func=ACT.Relu)

        def load_rows(rows, dram, first, count):
            tiles = slice(first, first + count)
            nc.sync.dma_start(out=rows[:, tiles, :], in_=dram[:, tiles, :])

        def load_words(words, words_dram):
            nc.sync.dma_start(
                out=words[:].bitcast(I32), in_=words_dram.rearrange("g p n t -> (g p) (n t)").bitcast(I32)
            )

        def load_scales(scales, scales_dram):
            for q in range(QUADRANTS):
                nc.sync.dma_start(
                    out=scales[32 * q : 32 * q + 4, :].bitcast(I32),
                    in_=scales_dram[0, 4 * q : 4 * q + 4, :].bitcast(I32),
                )

        load_rows(o_rows, o_dram, 0, 2)
        load_scales(wo_scales, W_O_scales)
        load_words(wo_words, W_O_words)
        load_rows(xn_rows, xn_dram, 0, 2)
        nc.sync.dma_start(out=factor_row[0:1, FFN : FFN + 1], in_=scale_ffn.unsqueeze(0))
        nc.sync.dma_start(out=bias_row[0:1, :], in_=ffn1_b.unsqueeze(0))
        load_rows(o_rows, o_dram, 2, 2)
        load_rows(xn_rows, xn_dram, 2, 2)
        load_words(w1_words, ffn1_w_words)
        load_scales(w1_scales, ffn1_w_scales)
        for first_tile in range(4, TILES, 2):
            load_rows(o_rows, o_dram, first_tile, 2)
            load_rows(xn_rows, xn_dram, first_tile, 2)

        factors = keep.tile([P, FACTORS], F32)

        def spread_factor(first):
            cols = slice(first, first + 32)
            spread = psum_back.tile([P, 32], F32, name="back")
            nc.tensor.matmul(spread[:], lhsT=ones[:], rhs=factor_row[:, cols], start=True, stop=True)
            nc.scalar.copy(out=factors[:, cols], in_=spread[:])

        attn = factors[:, ATTN : ATTN + 1]
        ffn = factors[:, FFN : FFN + 1]

        bias_all = keep.tile([P, DIRECT], F32)

        spreads = {}

        def spread_bias(bank, spread):
            cols = slice(bank * BANK, (bank + 1) * BANK)
            spreads[bank] = spread
            nc.tensor.matmul(spread[:], lhsT=ones[:], rhs=bias_row[:, cols], start=True, stop=True)

        def spread_out(bank):
            cols = slice(bank * BANK, (bank + 1) * BANK)
            nc.scalar.activation(out=bias_all[:, cols], in_=spreads[bank][:], func=ACT.Copy, scale=ffn)

        bias_turned = keep.tile([P, BLOCKS], F32)

        def turn_bias():
            column = psum_turn.tile([P, BLOCKS], F32, name="turned")
            for c in range(BLOCKS):
                nc.tensor.matmul(
                    column[:, c : c + 1],
                    lhsT=bias_row[:, DIRECT + c * P : DIRECT + (c + 1) * P],
                    rhs=ones[:, 0:1],
                    start=True,
                    stop=True,
                )
            nc.scalar.activation(out=bias_turned[:], in_=column[:], func=ACT.Copy, scale=ffn)

        def turn(rows, j, turned=None):
            if turned is None:
                turned = psum_turn.tile([P, 2, P], F32)
            words = rows[:, j, :].bitcast(F32)
            for u in range(2):
                nc.tensor.transpose(turned[:, u, :], words[:, u : K // 2 : 2], identity[:])
            return turned

        def o_unit(j):
            return 2 * j

        def y_unit(j):
            return 2 * (j + Y_LAG) + 1

        def quantise_unit(unit):
            nc.vector.quantize_mx(
                out=words[:, unit * P : (unit + 1) * P].bitcast(FP8X4),
                scales=scales[:, unit * P : (unit + 1) * P],
                in_=grouped[:, unit * K : (unit + 1) * K],
            )

        def quantise(step):
            first = o_unit(step) if step < TILES else y_unit(step - Y_LAG)
            last = y_unit(step - Y_LAG) if step >= Y_LAG else o_unit(step)
            nc.vector.quantize_mx(
                out=words[:, first * P : (last + 1) * P].bitcast(FP8X4),
                scales=scales[:, first * P : (last + 1) * P],
                in_=grouped[:, first * K : (last + 1) * K],
            )

        o_turned, y_turned, y_sums, h_sums, t_sums, h_tiles, t_tiles, backs = {}, {}, {}, {}, {}, {}, {}, {}

        def o_turn(j, *where):
            o_turned[j] = turn(o_rows, j, *where)

        def o_copy(j):
            nc.scalar.copy(
                out=grouped[:, o_unit(j) * K : (o_unit(j) + 1) * K].bitcast(F32).rearrange("p (r u) -> p r u", u=2),
                in_=o_turned[j][:].rearrange("p u r -> p r u"),
            )

        def attention_pass(j):
            tokens = slice(o_unit(j) * P, (o_unit(j) + 1) * P)
            if j in (1, 3):
                acc_y = psum_t.tile([P, BLOCKS, P], F32, name="acc_t")[:].rearrange("p c r -> p (c r)")
            else:
                acc_y = psum_y.tile([P, CH], F32)
            y_sums[j] = acc_y
            nc.tensor.matmul_mx(
                out=acc_y[:],
                lhsT=words[:, tokens].bitcast(FP8X4),
                lhsT_scale=scales[:, tokens],
                rhs=wo_words[:].bitcast(FP8X4),
                rhs_scale=wo_scales[:],
                start=True,
                stop=True,
            )

        def attention_add(j):
            nc.vector.scalar_tensor_tensor(
                out=y_rows[:, j, :],
                in0=y_sums[j][:],
                scalar=attn,
                in1=xn_rows[:, j, :],
                op0=ALU.mult,
                op1=ALU.add,
            )

        def y_turn(j):
            y_turned[j] = turn(y_rows, j)

        def y_copy(j):
            nc.scalar.activation(
                out=grouped[:, y_unit(j) * K : (y_unit(j) + 1) * K].rearrange("p (r u e) -> p r u e", u=2, e=2),
                in_=y_turned[j][:].bitcast(BF16).rearrange("p u (r e) -> p r u e", e=2),
                func=ACT.Relu,
            )

        def direct_pass(j, bank):
            tokens = slice(y_unit(j) * P, (y_unit(j) + 1) * P)
            cols = slice(bank * BANK, (bank + 1) * BANK)
            acc_h = psum_h.tile([P, BANK], F32)
            h_sums[j, bank] = acc_h
            nc.tensor.matmul_mx(
                out=acc_h[:],
                lhsT=words[:, tokens].bitcast(FP8X4),
                lhsT_scale=scales[:, tokens],
                rhs=w1_words[:, cols].bitcast(FP8X4),
                rhs_scale=w1_scales[:, cols],
                start=True,
                stop=True,
            )

        def direct_passes(j):
            for bank in range(DIRECT // BANK):
                direct_pass(j, bank)

        def store(j, cols):
            nc.sync.dma_start(out=out_dram[:, j, cols], in_=h_tiles[j][:, cols])

        def rows_of_h(j):
            if j not in h_tiles:
                h = h_pool.tile([P, FF], F32)
                h_tiles[j] = h
            return h_tiles[j]

        def direct_out(j, bank):
            h = rows_of_h(j)
            cols = slice(bank * BANK, (bank + 1) * BANK)
            nc.vector.scalar_tensor_tensor(
                out=h[:, cols],
                in0=h_sums[j, bank][:],
                scalar=ffn,
                in1=bias_all[:, cols],
                op0=ALU.mult,
                op1=ALU.add,
            )
            if bank < POOL_BANKS or j == 0:
                nc.gpsimd.tensor_scalar(
                    out=h[:, cols], in0=h[:, cols], scalar1=LARGEST, scalar2=0.0, op0=ALU.min, op1=ALU.max
                )
            else:
                nc.scalar.activation(out=h[:, cols], in_=h[:, cols], func=ACT.Relu)
            if j > 0:
                if bank == 1:
                    store(j, slice(0, 2 * BANK))
            else:
                store(j, cols)

        def turned_passes(j):
            tokens = slice(y_unit(j) * P, (y_unit(j) + 1) * P)
            acc_t = psum_t.tile([P, BLOCKS, P], F32)
            t_sums[j] = acc_t
            for c in range(BLOCKS):
                cols = slice(DIRECT + c * P, DIRECT + (c + 1) * P)
                nc.tensor.matmul_mx(
                    out=acc_t[:, c, :],
                    lhsT=w1_words[:, cols].bitcast(FP8X4),
                    lhsT_scale=w1_scales[:, cols],
                    rhs=words[:, tokens].bitcast(FP8X4),
                    rhs_scale=scales[:, tokens],
                    start=True,
                    stop=True,
                )

        def turned_out(j):
            h_turned = t_pool.tile([P, BLOCKS, P], F32)
            t_tiles[j] = h_turned
            for c in range(BLOCKS):
                nc.scalar.activation(
                    out=h_turned[:, c, :],
                    in_=t_sums[j][:, c, :],
                    func=ACT.Relu,
                    bias=bias_turned[:, c : c + 1],
                    scale=ffn,
                )

        def back_turn(j):
            back = psum_back.tile([P, BLOCKS, P], F32)
            backs[j] = back
            for c in range(BLOCKS):
                nc.tensor.transpose(back[:, c, :], t_tiles[j][:, c, :], identity[:])

        def back_copy(j):
            h = rows_of_h(j)
            nc.scalar.copy(out=h[:, DIRECT:FF], in_=backs[j][:].rearrange("p c r -> p (c r)"))
            if j == 0:
                store(j, slice(DIRECT, FF))

        def stage(function, j, *rest):
            if 0 <= j < TILES:
                function(j, *rest)

        ctx.enter_context(
            tc.manual_schedule(engines={mybir.EngineType.PE, mybir.EngineType.DVE, mybir.EngineType.Activation})
        )
        for j in range(2):
            o_turn(j)
            o_copy(j)
            quantise_unit(o_unit(j))
        spread_factor(ATTN)
        attention_pass(0)
        attention_pass(1)
        o_turn(2, psum_h.tile([P, 2, P], F32, name="acc_h"))
        o_copy(2)
        attention_add(0)
        attention_add(1)
        o_turn(3, psum_back.tile([P, 2, P], F32, name="back"))
        o_copy(3)
        y_turn(0)
        y_copy(0)
        y_turn(1)
        y_copy(1)
        quantise_unit(o_unit(2))
        quantise_unit(o_unit(3))
        spread_factor(FFN)
        spread_bias(0, psum_h.tile([P, BANK], F32, name="acc_h"))
        attention_pass(2)
        spread_out(0)
        spread_bias(1, psum_h.tile([P, BANK], F32, name="acc_h"))
        spread_out(1)
        quantise_unit(y_unit(0))
        direct_pass(0, 0)
        attention_pass(3)
        attention_add(2)
        spread_bias(2, psum_back.tile([P, BANK], F32, name="back"))
        spread_out(2)
        turn_bias()
        quantise_unit(y_unit(1))
        direct_out(0, 0)
        attention_add(3)
        direct_pass(0, 1)
        direct_pass(0, 2)
        y_turn(2)
        y_copy(2)
        o_turn(4)
        o_copy(4)
        turned_passes(0)
        turned_out(0)
        direct_pass(1, 0)
        direct_out(0, 1)
        direct_pass(1, 1)
        direct_out(0, 2)
        quantise(4)
        back_turn(0)
        back_copy(0)
        direct_pass(1, 2)
        turned_passes(1)
        attention_pass(4)
        turned_out(1)

        for step in range(5, TILES + 4):
            stage(y_turn, step - 2)
            stage(o_turn, step)
            stage(back_turn, step - 4)
            stage(y_copy, step - 2)
            stage(o_copy, step)
            stage(back_copy, step - 4)
            if step > 5:
                stage(attention_pass, step - 1)
            stage(turned_passes, step - 3)
            stage(turned_out, step - 3)
            for bank in range(DIRECT // BANK):
                stage(direct_out, step - 4, bank)
            j = step - 4
            if 0 < j < TILES:
                store(j, slice(2 * BANK, FF))
            for bank in range(DIRECT // BANK):
                stage(direct_pass, step - 3, bank)
            stage(attention_add, step - 1)
            if step < TILES + Y_LAG:
                quantise(step)
